import numpy as np
import ml_dtypes


def mxq(x, axis, fmt="e4m3"):
    dtype, down = {"e4m3": (ml_dtypes.float8_e4m3fn, 7), "e5m2": (ml_dtypes.float8_e5m2, 14)}[fmt]
    v = np.moveaxis(np.asarray(x, np.float32).astype(ml_dtypes.bfloat16).astype(np.float64), axis, -1)
    blocks = v.reshape(v.shape[:-1] + (-1, 32))
    amax = np.abs(blocks).max(-1, keepdims=True)
    byte = np.maximum(np.where(amax > 0, np.frexp(amax)[1] - 1 + 127, 0) - down, 1)
    scale = np.exp2(byte - 127.0)
    codes = (blocks / scale).astype(np.float32).astype(dtype).astype(np.float64)
    return np.moveaxis((codes * scale).reshape(v.shape), -1, axis)


WIDE = False


def mx_kscale(k):
    if not WIDE:
        return np.ones(k)
    levels = np.array([10, -10, 5, -5, 0])
    a = np.random.permutation(np.resize(levels, k // 512 * 4)).reshape(k // 512, 4)
    idx = np.arange(k)
    return np.exp2(a[idx // 512, idx % 128 // 32])


BF16 = ml_dtypes.bfloat16


def bf(x):
    return np.asarray(x, np.float32).astype(BF16)


def f64(x):
    return np.asarray(x).astype(np.float64)


B, CH, C1, C2, D, NF, W, H = 1, 1024, 128, 512, 2, 8, 16, 16
N = NF * W * H
M = NF * (W // D) * (H // D)


def setup_inputs():
    t = mx_kscale(C2)
    return {"theta": bf(np.tanh(np.random.standard_normal((B, N, C1)) * 0.3)),
            "phi": bf(np.tanh(0.3 + np.random.standard_normal((B, M, C1)) * 0.2)),
            "g": bf((1.0 + np.random.standard_normal((B, M, C2)) * 0.7) * t),
            "x": bf(np.random.standard_normal((B, CH, NF, W, H))),
            "w_attn_g": bf(np.random.standard_normal((CH, C2)) * 2.0 / np.sqrt(C2) / t),
            "b_attn_g": bf(np.random.standard_normal(CH) * 0.2),
            "gamma": bf(0.6 + np.random.standard_normal(1) * 0.2)}


def reference(theta, phi, g, x, w_attn_g, b_attn_g, gamma):
    s = f64(theta) @ f64(phi).transpose(0, 2, 1)
    e = np.exp(s - s.max(axis=1, keepdims=True))
    attn = e / e.sum(axis=1, keepdims=True)
    a = mxq(attn, 2, "e4m3") @ mxq(f64(g), 1, "e4m3")
    y = (mxq(f64(w_attn_g), 1, "e4m3") @ mxq(a.transpose(0, 2, 1), 1, "e4m3")) + f64(b_attn_g)[None, :, None]
    attn_g = y.reshape(B, CH, NF, W, H)
    alpha = 1.0 / (1.0 + np.exp(-f64(gamma)[0]))
    out = (1.0 - alpha) * f64(x) + alpha * attn_g
    return out, attn_g

@@ -1,0 +1,243 @@
+from contextlib import ExitStack
+
+import concourse.mybir as mybir
+from concourse.masks import make_identity
+
+F32 = mybir.dt.float32
+BF16 = mybir.dt.bfloat16
+U32 = mybir.dt.uint32
+U8 = mybir.dt.uint8
+FP8X4 = mybir.dt.float8_e4m3fn_x4
+ACT = mybir.ActivationFunctionType
+ALU = mybir.AluOpType
+AX = mybir.AxisListType
+
+P = 128
+PACK = 4
+BANK = 512
+QUERIES = 2048
+KEYS = 512
+C_QK = 128
+C_V = 512
+CH = 1024
+CHUNKS = QUERIES // BANK
+CH_TILES = CH // P
+
+FLOPS = 2 * QUERIES * KEYS * C_QK + 2 * QUERIES * KEYS * C_V + 2 * CH * C_V * QUERIES
+
+
+def tile_selfattention3d_pa_kernel(
+    tc, theta, phi, g, x, w_attn_g, b_attn_g, gamma, out_0, out_1
+):
+    nc = tc.nc
+    with ExitStack() as ctx:
+        keep = ctx.enter_context(tc.tile_pool(name="keep", bufs=1))
+        work = ctx.enter_context(tc.tile_pool(name="work", bufs=2))
+        stage = ctx.enter_context(tc.tile_pool(name="stage", bufs=4))
+        psum = ctx.enter_context(tc.psum_pool(name="psum", bufs=8))
+
+        phi_sb = keep.tile([P, PACK, C_QK], BF16)
+        nc.sync.dma_start(out=phi_sb[:], in_=phi.rearrange("b (p t) k -> (b p) t k", t=PACK))
+        theta_sb = keep.tile([P, CHUNKS, PACK, C_QK], BF16)
+        theta_view = theta.rearrange("b (c j p) k -> (b c) p j k", j=PACK, p=P)
+        for c in range(CHUNKS):
+            nc.sync.dma_start(out=theta_sb[:, c, :, :], in_=theta_view[c])
+        g_raw = keep.tile([P, PACK, C_V], BF16)
+        nc.sync.dma_start(out=g_raw[:], in_=g.rearrange("b (p j) w -> (b p) j w", j=PACK))
+        w_sb = keep.tile([P, CH_TILES, C_V], BF16)
+        nc.sync.dma_start(out=w_sb[:], in_=w_attn_g.rearrange("(h p) k -> p h k", p=P))
+        x_sb = keep.tile([P, CH_TILES, QUERIES], BF16)
+        x_view = x.rearrange("b (h p) f r c -> (b h) p (f r c)", p=P)
+        for h in range(CH_TILES):
+            nc.sync.dma_start(out=x_sb[:, h, :], in_=x_view[h])
+
+        gamma_sb = keep.tile([P, 1], BF16)
+        nc.scalar.dma_start(out=gamma_sb[:], in_=gamma.partition_broadcast(P))
+        b_rows = keep.tile([P, P], BF16)
+        nc.vector.memset(b_rows[:], 0.0)
+        nc.scalar.dma_start(out=b_rows[0:CH_TILES, :], in_=b_attn_g.rearrange("(h p) -> h p", p=P))
+
+        ident_bf = keep.tile([P, P], BF16)
+        make_identity(nc, ident_bf[:])
+        ident_f32 = keep.tile([P, P], F32)
+        make_identity(nc, ident_f32[:])
+
+        exp_neg = keep.tile([P, 1], F32)
+        nc.scalar.activation(out=exp_neg[:], in_=gamma_sb[:], func=ACT.Exp, scale=-1.0)
+        alpha = keep.tile([P, 1], F32)
+        nc.vector.tensor_scalar_add(out=alpha[:], in0=exp_neg[:], scalar1=1.0)
+        nc.vector.reciprocal(out=alpha[:], in_=alpha[:])
+        one_minus = keep.tile([P, 1], F32)
+        nc.vector.tensor_scalar(
+            out=one_minus[:], in0=alpha[:], scalar1=-1.0, scalar2=1.0, op0=ALU.mult, op1=ALU.add
+        )
+
+        phiT = keep.tile([P, PACK, P], BF16)
+        phiT_ps = psum.tile([P, PACK, P], BF16, tag="bank")
+        for t in range(PACK):
+            nc.tensor.transpose(phiT_ps[:, t, :], phi_sb[:, t, :], ident_bf[:])
+        nc.vector.tensor_copy(out=phiT[:], in_=phiT_ps[:])
+
+        thetaT = keep.tile([P, CHUNKS, PACK, P], BF16)
+        for c in range(CHUNKS):
+            thetaT_ps = psum.tile([P, PACK, P], BF16, tag="bank")
+            for j in range(PACK):
+                nc.tensor.transpose(thetaT_ps[:, j, :], theta_sb[:, c, j, :], ident_bf[:])
+            if c % 2 == 0:
+                nc.scalar.copy(out=thetaT[:, c, :, :], in_=thetaT_ps[:])
+            else:
+                nc.vector.tensor_copy(out=thetaT[:, c, :, :], in_=thetaT_ps[:])
+
+        bT_ps = psum.tile([P, P], BF16, tag="bank")
+        nc.tensor.transpose(bT_ps[:], b_rows[:], ident_bf[:])
+        b_col = keep.tile([P, CH_TILES], F32)
+        nc.vector.tensor_copy(out=b_col[:], in_=bT_ps[:, 0:CH_TILES])
+        alpha_b = keep.tile([P, CH_TILES], F32)
+        nc.vector.tensor_scalar_mul(out=alpha_b[:], in0=b_col[:], scalar1=alpha[:, 0:1])
+
+        g_grouped = keep.tile([P, PACK, P, PACK], BF16, align_bytes=64)
+        nc.vector.tensor_copy(out=g_grouped[:], in_=g_raw[:].rearrange("p j (h t) -> p t h j", t=PACK))
+        g_codes = keep.tile([P, C_V], U32, align_bytes=64)
+        g_scales = keep.tile([P, C_V], U8, align_bytes=64)
+        nc.vector.quantize_mx(
+            out=g_codes[:].bitcast(FP8X4),
+            scales=g_scales[:],
+            in_=g_grouped[:].rearrange("p t h j -> p (t h j)"),
+        )
+
+        mix = keep.tile([P, CH_TILES, QUERIES], F32)
+        for c in range(CHUNKS):
+            cols = slice(c * BANK, (c + 1) * BANK)
+            for h in range(CH_TILES):
+                nc.gpsimd.tensor_scalar(
+                    out=mix[:, h, cols],
+                    in0=x_sb[:, h, cols],
+                    scalar1=one_minus[:, 0:1],
+                    scalar2=alpha_b[:, h : h + 1],
+                    op0=ALU.mult,
+                    op1=ALU.add,
+                )
+
+        e = keep.tile([P, PACK, QUERIES], F32)
+        bank_max = keep.tile([P, PACK, CHUNKS], F32)
+        neg_max = keep.tile([P, PACK], F32)
+        bank_sum = keep.tile([P, PACK, CHUNKS], F32)
+        key_sum = keep.tile([P, PACK], F32)
+        recip = keep.tile([P, PACK], F32)
+        for t in range(PACK):
+            s_banks = []
+            for c in range(CHUNKS):
+                s_ps = psum.tile([P, BANK], F32, tag="bank", name="s_ps")
+                nc.tensor.matmul(
+                    s_ps[:],
+                    lhsT=phiT[:, t, :],
+                    rhs=thetaT[:, c, :, :].rearrange("k j p -> k (j p)"),
+                    start=True,
+                    stop=True,
+                )
+                nc.vector.reduce_max(out=bank_max[:, t, c : c + 1], in_=s_ps[:], axis=AX.X)
+                s_banks.append(s_ps)
+            nc.vector.tensor_reduce(
+                out=neg_max[:, t : t + 1], in_=bank_max[:, t, :], axis=AX.X, op=ALU.max, negate=True
+            )
+            for c in range(CHUNKS):
+                nc.scalar.activation(
+                    out=e[:, t, c * BANK : (c + 1) * BANK],
+                    in_=s_banks[c][:],
+                    func=ACT.Exp,
+                    bias=neg_max[:, t : t + 1],
+                    scale=1.0,
+                    accum_out=bank_sum[:, t, c : c + 1],
+                )
+            nc.vector.reduce_sum(out=key_sum[:, t : t + 1], in_=bank_sum[:, t, :], axis=AX.X)
+            nc.vector.reciprocal(out=recip[:, t : t + 1], in_=key_sum[:, t : t + 1])
+
+        w_grouped = keep.tile([P, CH, PACK], BF16, align_bytes=64)
+        w_words = w_grouped[:].bitcast(F32)
+        for pair in range(CH_TILES // 2):
+            wT_ps = psum.tile([P, 2, 2 * P], F32, tag="bank")
+            for i in range(2):
+                words = w_sb[:, 2 * pair + i, :].bitcast(F32).rearrange("p (q u) -> p u q", u=2)
+                for u in range(2):
+                    nc.tensor.transpose(wT_ps[:, u, i * P : (i + 1) * P], words[:, u, :], ident_f32[:])
+            nc.vector.tensor_copy(
+                out=w_words[:, 2 * pair * P : (2 * pair + 2) * P, :],
+                in_=wT_ps[:].rearrange("q u h -> q h u"),
+            )
+        w_codes = keep.tile([P, CH], U32, align_bytes=64)
+        w_scales = keep.tile([P, CH], U8, align_bytes=64)
+        nc.vector.quantize_mx(
+            out=w_codes[:].bitcast(FP8X4),
+            scales=w_scales[:],
+            in_=w_grouped[:].rearrange("p h t -> p (h t)"),
+        )
+
+        attn_codes = keep.tile([P, QUERIES], U32, align_bytes=64)
+        attn_scales = keep.tile([P, QUERIES], U8, align_bytes=64)
+        a_codes = keep.tile([P, QUERIES], U32, align_bytes=64)
+        a_scales = keep.tile([P, QUERIES], U8, align_bytes=64)
+        out_view = out_0.rearrange("b (h p) f r c -> (b h) p (f r c)", p=P)
+        attn_g_view = out_1.rearrange("b (h p) f r c -> (b h) p (f r c)", p=P)
+
+        for c in range(CHUNKS):
+            cols = slice(c * BANK, (c + 1) * BANK)
+            attn_grouped = work.tile([P, BANK, PACK], BF16, align_bytes=64)
+            nc.vector.tensor_tensor(
+                out=attn_grouped[:],
+                in0=e[:, :, cols].rearrange("p t n -> p n t"),
+                in1=recip[:].unsqueeze(1).to_broadcast([P, BANK, PACK]),
+                op=ALU.mult,
+            )
+            nc.vector.quantize_mx(
+                out=attn_codes[:, cols].bitcast(FP8X4),
+                scales=attn_scales[:, cols],
+                in_=attn_grouped[:].rearrange("p n t -> p (n t)"),
+            )
+            a_grouped = work.tile([P, BANK, PACK], BF16, align_bytes=64)
+            for nb in range(BANK // P):
+                n0 = c * BANK + nb * P
+                a_ps = psum.tile([P, PACK, P], F32, tag="bank")
+                for t in range(PACK):
+                    nc.tensor.matmul_mx(
+                        out=a_ps[:, t, :],
+                        lhsT=g_codes[:, t * P : (t + 1) * P].bitcast(FP8X4),
+                        lhsT_scale=g_scales[:, t * P : (t + 1) * P],
+                        rhs=attn_codes[:, n0 : n0 + P].bitcast(FP8X4),
+                        rhs_scale=attn_scales[:, n0 : n0 + P],
+                        start=True,
+                        stop=True,
+                    )
+                nc.scalar.copy(
+                    out=a_grouped[:, nb * P : (nb + 1) * P, :],
+                    in_=a_ps[:].rearrange("p t n -> p n t"),
+                )
+            nc.vector.quantize_mx(
+                out=a_codes[:, cols].bitcast(FP8X4),
+                scales=a_scales[:, cols],
+                in_=a_grouped[:].rearrange("p n t -> p (n t)"),
+            )
+            for h in range(CH_TILES):
+                y_ps = psum.tile([P, BANK], F32, tag="bank")
+                nc.tensor.matmul_mx(
+                    out=y_ps[:],
+                    lhsT=w_codes[:, h * P : (h + 1) * P].bitcast(FP8X4),
+                    lhsT_scale=w_scales[:, h * P : (h + 1) * P],
+                    rhs=a_codes[:, cols].bitcast(FP8X4),
+                    rhs_scale=a_scales[:, cols],
+                    start=True,
+                    stop=True,
+                )
+                attn_g_sb = stage.tile([P, BANK], F32)
+                nc.scalar.activation(
+                    out=attn_g_sb[:], in_=y_ps[:], func=ACT.Identity, bias=b_col[:, h : h + 1], scale=1.0
+                )
+                nc.sync.dma_start(out=attn_g_view[h][:, cols], in_=attn_g_sb[:])
+                nc.vector.scalar_tensor_tensor(
+                    out=mix[:, h, cols],
+                    in0=y_ps[:],
+                    scalar=alpha[:, 0:1],
+                    in1=mix[:, h, cols],
+                    op0=ALU.mult,
+                    op1=ALU.add,
+                )
+                nc.sync.dma_start(out=out_view[h][:, cols], in_=mix[:, h, cols])

@@ -22,6 +22,9 @@ C_V = 512
 CH = 1024
 CHUNKS = QUERIES // BANK
 CH_TILES = CH // P
+BLOCKS = BANK // P
+PSUM_BANKS = 8
+STAGE_BUFS = 8
 
 FLOPS = 2 * QUERIES * KEYS * C_QK + 2 * QUERIES * KEYS * C_V + 2 * CH * C_V * QUERIES
 
@@ -33,8 +36,9 @@ def tile_selfattention3d_pa_kernel(
     with ExitStack() as ctx:
         keep = ctx.enter_context(tc.tile_pool(name="keep", bufs=1))
         work = ctx.enter_context(tc.tile_pool(name="work", bufs=2))
-        stage = ctx.enter_context(tc.tile_pool(name="stage", bufs=4))
-        psum = ctx.enter_context(tc.psum_pool(name="psum", bufs=8))
+        stage = ctx.enter_context(tc.tile_pool(name="stage", bufs=STAGE_BUFS))
+        psum = ctx.enter_context(tc.psum_pool(name="psum", bufs=PSUM_BANKS))
+        ctx.enter_context(tc.manual_schedule())
 
         phi_sb = keep.tile([P, PACK, C_QK], BF16)
         nc.sync.dma_start(out=phi_sb[:], in_=phi.rearrange("b (p t) k -> (b p) t k", t=PACK))
@@ -92,38 +96,14 @@ def tile_selfattention3d_pa_kernel(
         nc.tensor.transpose(bT_ps[:], b_rows[:], ident_bf[:])
         b_col = keep.tile([P, CH_TILES], F32)
         nc.vector.tensor_copy(out=b_col[:], in_=bT_ps[:, 0:CH_TILES])
-        alpha_b = keep.tile([P, CH_TILES], F32)
-        nc.vector.tensor_scalar_mul(out=alpha_b[:], in0=b_col[:], scalar1=alpha[:, 0:1])
 
         g_grouped = keep.tile([P, PACK, P, PACK], BF16, align_bytes=64)
-        nc.vector.tensor_copy(out=g_grouped[:], in_=g_raw[:].rearrange("p j (h t) -> p t h j", t=PACK))
-        g_codes = keep.tile([P, C_V], U32, align_bytes=64)
-        g_scales = keep.tile([P, C_V], U8, align_bytes=64)
-        nc.vector.quantize_mx(
-            out=g_codes[:].bitcast(FP8X4),
-            scales=g_scales[:],
-            in_=g_grouped[:].rearrange("p t h j -> p (t h j)"),
-        )
-
-        mix = keep.tile([P, CH_TILES, QUERIES], F32)
-        for c in range(CHUNKS):
-            cols = slice(c * BANK, (c + 1) * BANK)
-            for h in range(CH_TILES):
-                nc.gpsimd.tensor_scalar(
-                    out=mix[:, h, cols],
-                    in0=x_sb[:, h, cols],
-                    scalar1=one_minus[:, 0:1],
-                    scalar2=alpha_b[:, h : h + 1],
-                    op0=ALU.mult,
-                    op1=ALU.add,
-                )
+        nc.scalar.copy(out=g_grouped[:], in_=g_raw[:].rearrange("p j (h t) -> p t h j", t=PACK))
 
         e = keep.tile([P, PACK, QUERIES], F32)
         bank_max = keep.tile([P, PACK, CHUNKS], F32)
         neg_max = keep.tile([P, PACK], F32)
         bank_sum = keep.tile([P, PACK, CHUNKS], F32)
-        key_sum = keep.tile([P, PACK], F32)
-        recip = keep.tile([P, PACK], F32)
         for t in range(PACK):
             s_banks = []
             for c in range(CHUNKS):
@@ -149,8 +129,14 @@ def tile_selfattention3d_pa_kernel(
                     scale=1.0,
                     accum_out=bank_sum[:, t, c : c + 1],
                 )
-            nc.vector.reduce_sum(out=key_sum[:, t : t + 1], in_=bank_sum[:, t, :], axis=AX.X)
-            nc.vector.reciprocal(out=recip[:, t : t + 1], in_=key_sum[:, t : t + 1])
+
+        g_codes = keep.tile([P, C_V], U32, align_bytes=64)
+        g_scales = keep.tile([P, C_V], U8, align_bytes=64)
+        nc.vector.quantize_mx(
+            out=g_codes[:].bitcast(FP8X4),
+            scales=g_scales[:],
+            in_=g_grouped[:].rearrange("p t h j -> p (t h j)"),
+        )
 
         w_grouped = keep.tile([P, CH, PACK], BF16, align_bytes=64)
         w_words = w_grouped[:].bitcast(F32)
@@ -166,78 +152,135 @@ def tile_selfattention3d_pa_kernel(
             )
         w_codes = keep.tile([P, CH], U32, align_bytes=64)
         w_scales = keep.tile([P, CH], U8, align_bytes=64)
-        nc.vector.quantize_mx(
-            out=w_codes[:].bitcast(FP8X4),
-            scales=w_scales[:],
-            in_=w_grouped[:].rearrange("p h t -> p (h t)"),
-        )
+
+        key_sum = keep.tile([P, PACK], F32)
+        recip = keep.tile([P, PACK], F32)
+        nc.vector.reduce_sum(out=key_sum[:], in_=bank_sum[:], axis=AX.X)
+        nc.vector.reciprocal(out=recip[:], in_=key_sum[:])
 
         attn_codes = keep.tile([P, QUERIES], U32, align_bytes=64)
         attn_scales = keep.tile([P, QUERIES], U8, align_bytes=64)
         a_codes = keep.tile([P, QUERIES], U32, align_bytes=64)
         a_scales = keep.tile([P, QUERIES], U8, align_bytes=64)
+        mix = keep.tile([P, CH_TILES, QUERIES], F32)
         out_view = out_0.rearrange("b (h p) f r c -> (b h) p (f r c)", p=P)
         attn_g_view = out_1.rearrange("b (h p) f r c -> (b h) p (f r c)", p=P)
+        attn_grouped = {}
+        a_grouped = {}
 
-        for c in range(CHUNKS):
-            cols = slice(c * BANK, (c + 1) * BANK)
-            attn_grouped = work.tile([P, BANK, PACK], BF16, align_bytes=64)
+        def chunk_cols(c):
+            return slice(c * BANK, (c + 1) * BANK)
+
+        def normalise(c):
+            attn_grouped[c] = work.tile([P, BANK, PACK], BF16, align_bytes=64, name="attn_grouped")
             nc.vector.tensor_tensor(
-                out=attn_grouped[:],
-                in0=e[:, :, cols].rearrange("p t n -> p n t"),
+                out=attn_grouped[c][:],
+                in0=e[:, :, chunk_cols(c)].rearrange("p t n -> p n t"),
                 in1=recip[:].unsqueeze(1).to_broadcast([P, BANK, PACK]),
                 op=ALU.mult,
             )
+
+        def quantise_attn(c):
             nc.vector.quantize_mx(
-                out=attn_codes[:, cols].bitcast(FP8X4),
-                scales=attn_scales[:, cols],
-                in_=attn_grouped[:].rearrange("p n t -> p (n t)"),
+                out=attn_codes[:, chunk_cols(c)].bitcast(FP8X4),
+                scales=attn_scales[:, chunk_cols(c)],
+                in_=attn_grouped[c][:].rearrange("p n t -> p (n t)"),
             )
-            a_grouped = work.tile([P, BANK, PACK], BF16, align_bytes=64)
-            for nb in range(BANK // P):
-                n0 = c * BANK + nb * P
-                a_ps = psum.tile([P, PACK, P], F32, tag="bank")
-                for t in range(PACK):
-                    nc.tensor.matmul_mx(
-                        out=a_ps[:, t, :],
-                        lhsT=g_codes[:, t * P : (t + 1) * P].bitcast(FP8X4),
-                        lhsT_scale=g_scales[:, t * P : (t + 1) * P],
-                        rhs=attn_codes[:, n0 : n0 + P].bitcast(FP8X4),
-                        rhs_scale=attn_scales[:, n0 : n0 + P],
-                        start=True,
-                        stop=True,
-                    )
-                nc.scalar.copy(
-                    out=a_grouped[:, nb * P : (nb + 1) * P, :],
-                    in_=a_ps[:].rearrange("p t n -> p n t"),
-                )
-            nc.vector.quantize_mx(
-                out=a_codes[:, cols].bitcast(FP8X4),
-                scales=a_scales[:, cols],
-                in_=a_grouped[:].rearrange("p n t -> p (n t)"),
-            )
-            for h in range(CH_TILES):
-                y_ps = psum.tile([P, BANK], F32, tag="bank")
+
+        def attend(c, nb):
+            if nb == 0:
+                a_grouped[c] = work.tile([P, BANK, PACK], BF16, align_bytes=64, name="a_grouped")
+            n0 = c * BANK + nb * P
+            a_ps = psum.tile([P, PACK, P], F32, tag="bank")
+            for t in range(PACK):
                 nc.tensor.matmul_mx(
-                    out=y_ps[:],
-                    lhsT=w_codes[:, h * P : (h + 1) * P].bitcast(FP8X4),
-                    lhsT_scale=w_scales[:, h * P : (h + 1) * P],
-                    rhs=a_codes[:, cols].bitcast(FP8X4),
-                    rhs_scale=a_scales[:, cols],
+                    out=a_ps[:, t, :],
+                    lhsT=g_codes[:, t * P : (t + 1) * P].bitcast(FP8X4),
+                    lhsT_scale=g_scales[:, t * P : (t + 1) * P],
+                    rhs=attn_codes[:, n0 : n0 + P].bitcast(FP8X4),
+                    rhs_scale=attn_scales[:, n0 : n0 + P],
                     start=True,
                     stop=True,
                 )
-                attn_g_sb = stage.tile([P, BANK], F32)
+            nc.scalar.copy(
+                out=a_grouped[c][:, nb * P : (nb + 1) * P, :],
+                in_=a_ps[:].rearrange("p t n -> p n t"),
+            )
+
+        def quantise_a(c):
+            nc.vector.quantize_mx(
+                out=a_codes[:, chunk_cols(c)].bitcast(FP8X4),
+                scales=a_scales[:, chunk_cols(c)],
+                in_=a_grouped[c][:].rearrange("p n t -> p (n t)"),
+            )
+
+        def scale_x(c, h):
+            if h % 2 == 0:
                 nc.scalar.activation(
-                    out=attn_g_sb[:], in_=y_ps[:], func=ACT.Identity, bias=b_col[:, h : h + 1], scale=1.0
+                    out=mix[:, h, chunk_cols(c)],
+                    in_=x_sb[:, h, chunk_cols(c)],
+                    func=ACT.Copy,
+                    scale=one_minus[:, 0:1],
                 )
-                nc.sync.dma_start(out=attn_g_view[h][:, cols], in_=attn_g_sb[:])
-                nc.vector.scalar_tensor_tensor(
-                    out=mix[:, h, cols],
-                    in0=y_ps[:],
-                    scalar=alpha[:, 0:1],
-                    in1=mix[:, h, cols],
-                    op0=ALU.mult,
-                    op1=ALU.add,
+            else:
+                nc.vector.tensor_scalar_mul(
+                    out=mix[:, h, chunk_cols(c)], in0=x_sb[:, h, chunk_cols(c)], scalar1=one_minus[:, 0:1]
                 )
-                nc.sync.dma_start(out=out_view[h][:, cols], in_=mix[:, h, cols])
+
+        def project(c, h):
+            y_ps = psum.tile([P, BANK], F32, tag="bank")
+            nc.tensor.matmul_mx(
+                out=y_ps[:],
+                lhsT=w_codes[:, h * P : (h + 1) * P].bitcast(FP8X4),
+                lhsT_scale=w_scales[:, h * P : (h + 1) * P],
+                rhs=a_codes[:, chunk_cols(c)].bitcast(FP8X4),
+                rhs_scale=a_scales[:, chunk_cols(c)],
+                start=True,
+                stop=True,
+            )
+            attn_g_sb = stage.tile([P, BANK], F32)
+            nc.scalar.activation(
+                out=attn_g_sb[:], in_=y_ps[:], func=ACT.Identity, bias=b_col[:, h : h + 1], scale=1.0
+            )
+            nc.sync.dma_start(out=attn_g_view[h][:, chunk_cols(c)], in_=attn_g_sb[:])
+            nc.vector.scalar_tensor_tensor(
+                out=mix[:, h, chunk_cols(c)],
+                in0=attn_g_sb[:],
+                scalar=alpha[:, 0:1],
+                in1=mix[:, h, chunk_cols(c)],
+                op0=ALU.mult,
+                op1=ALU.add,
+            )
+            nc.sync.dma_start(out=out_view[h][:, chunk_cols(c)], in_=mix[:, h, chunk_cols(c)])
+
+        normalise(0)
+        quantise_attn(0)
+        nc.vector.quantize_mx(
+            out=w_codes[:].bitcast(FP8X4),
+            scales=w_scales[:],
+            in_=w_grouped[:].rearrange("p h t -> p (h t)"),
+        )
+        for h in range(0, CH_TILES, 2):
+            scale_x(0, h)
+        for nb in range(BLOCKS):
+            attend(0, nb)
+        normalise(1)
+        quantise_a(0)
+        quantise_attn(1)
+        for h in range(1, CH_TILES, 2):
+            scale_x(0, h)
+
+        for c in range(CHUNKS):
+            for h in range(CH_TILES):
+                project(c, h)
+                if c + 1 < CHUNKS:
+                    scale_x(c + 1, h)
+                    if h < BLOCKS:
+                        attend(c + 1, h)
+                if h == BLOCKS - 1:
+                    if c + 2 < CHUNKS:
+                        normalise(c + 2)
+                    if c + 1 < CHUNKS:
+                        quantise_a(c + 1)
+                    if c + 2 < CHUNKS:
+                        quantise_attn(c + 2)

@@ -24,7 +24,8 @@ CHUNKS = QUERIES // BANK
 CH_TILES = CH // P
 BLOCKS = BANK // P
 PSUM_BANKS = 8
-STAGE_BUFS = 8
+STAGE_BUFS = 4
+PAIRS = CH_TILES // 2
 
 FLOPS = 2 * QUERIES * KEYS * C_QK + 2 * QUERIES * KEYS * C_V + 2 * CH * C_V * QUERIES
 
@@ -103,11 +104,10 @@ def tile_selfattention3d_pa_kernel(
         e = keep.tile([P, PACK, QUERIES], F32)
         bank_max = keep.tile([P, PACK, CHUNKS], F32)
         neg_max = keep.tile([P, PACK], F32)
-        bank_sum = keep.tile([P, PACK, CHUNKS], F32)
+        key_sum = keep.tile([P, PACK], F32)
         for t in range(PACK):
-            s_banks = []
             for c in range(CHUNKS):
-                s_ps = psum.tile([P, BANK], F32, tag="bank", name="s_ps")
+                s_ps = psum.tile([P, BANK], F32, tag="bank")
                 nc.tensor.matmul(
                     s_ps[:],
                     lhsT=phiT[:, t, :],
@@ -115,20 +115,26 @@ def tile_selfattention3d_pa_kernel(
                     start=True,
                     stop=True,
                 )
-                nc.vector.reduce_max(out=bank_max[:, t, c : c + 1], in_=s_ps[:], axis=AX.X)
-                s_banks.append(s_ps)
+                nc.vector.tensor_scalar(
+                    out=e[:, t, c * BANK : (c + 1) * BANK],
+                    in0=s_ps[:],
+                    scalar1=1.0,
+                    scalar2=None,
+                    op0=ALU.mult,
+                    op1=ALU.max,
+                    accum_out=bank_max[:, t, c : c + 1],
+                )
             nc.vector.tensor_reduce(
                 out=neg_max[:, t : t + 1], in_=bank_max[:, t, :], axis=AX.X, op=ALU.max, negate=True
             )
-            for c in range(CHUNKS):
-                nc.scalar.activation(
-                    out=e[:, t, c * BANK : (c + 1) * BANK],
-                    in_=s_banks[c][:],
-                    func=ACT.Exp,
-                    bias=neg_max[:, t : t + 1],
-                    scale=1.0,
-                    accum_out=bank_sum[:, t, c : c + 1],
-                )
+            nc.scalar.activation(
+                out=e[:, t, :],
+                in_=e[:, t, :],
+                func=ACT.Exp,
+                bias=neg_max[:, t : t + 1],
+                scale=1.0,
+                accum_out=key_sum[:, t : t + 1],
+            )
 
         g_codes = keep.tile([P, C_V], U32, align_bytes=64)
         g_scales = keep.tile([P, C_V], U8, align_bytes=64)
@@ -140,22 +146,26 @@ def tile_selfattention3d_pa_kernel(
 
         w_grouped = keep.tile([P, CH, PACK], BF16, align_bytes=64)
         w_words = w_grouped[:].bitcast(F32)
-        for pair in range(CH_TILES // 2):
+        for pair in range(PAIRS):
             wT_ps = psum.tile([P, 2, 2 * P], F32, tag="bank")
             for i in range(2):
                 words = w_sb[:, 2 * pair + i, :].bitcast(F32).rearrange("p (q u) -> p u q", u=2)
                 for u in range(2):
                     nc.tensor.transpose(wT_ps[:, u, i * P : (i + 1) * P], words[:, u, :], ident_f32[:])
-            nc.vector.tensor_copy(
-                out=w_words[:, 2 * pair * P : (2 * pair + 2) * P, :],
-                in_=wT_ps[:].rearrange("q u h -> q h u"),
-            )
+            if pair < PAIRS // 2:
+                nc.vector.tensor_copy(
+                    out=w_words[:, 2 * pair * P : (2 * pair + 2) * P, :],
+                    in_=wT_ps[:].rearrange("q u h -> q h u"),
+                )
+            else:
+                nc.scalar.copy(
+                    out=w_words[:, 2 * pair * P : (2 * pair + 2) * P, :],
+                    in_=wT_ps[:].rearrange("q u h -> q h u"),
+                )
         w_codes = keep.tile([P, CH], U32, align_bytes=64)
         w_scales = keep.tile([P, CH], U8, align_bytes=64)
 
-        key_sum = keep.tile([P, PACK], F32)
         recip = keep.tile([P, PACK], F32)
-        nc.vector.reduce_sum(out=key_sum[:], in_=bank_sum[:], axis=AX.X)
         nc.vector.reciprocal(out=recip[:], in_=key_sum[:])
 
         attn_codes = keep.tile([P, QUERIES], U32, align_bytes=64)
@@ -163,8 +173,8 @@ def tile_selfattention3d_pa_kernel(
         a_codes = keep.tile([P, QUERIES], U32, align_bytes=64)
         a_scales = keep.tile([P, QUERIES], U8, align_bytes=64)
         mix = keep.tile([P, CH_TILES, QUERIES], F32)
-        out_view = out_0.rearrange("b (h p) f r c -> (b h) p (f r c)", p=P)
-        attn_g_view = out_1.rearrange("b (h p) f r c -> (b h) p (f r c)", p=P)
+        out_view = out_0.rearrange("b (h p) f r c -> p (b h) (f r c)", p=P)
+        attn_g_view = out_1.rearrange("b (h p) f r c -> p (b h) (f r c)", p=P)
         attn_grouped = {}
         a_grouped = {}
 
@@ -214,44 +224,53 @@ def tile_selfattention3d_pa_kernel(
                 in_=a_grouped[c][:].rearrange("p n t -> p (n t)"),
             )
 
-        def scale_x(c, h):
-            if h % 2 == 0:
+        def pair_tiles(pair):
+            return slice(2 * pair, 2 * pair + 2)
+
+        def scale_x(c, pair):
+            if pair < PAIRS // 2:
+                nc.vector.tensor_scalar_mul(
+                    out=mix[:, pair_tiles(pair), chunk_cols(c)],
+                    in0=x_sb[:, pair_tiles(pair), chunk_cols(c)],
+                    scalar1=one_minus[:, 0:1],
+                )
+            else:
                 nc.scalar.activation(
-                    out=mix[:, h, chunk_cols(c)],
-                    in_=x_sb[:, h, chunk_cols(c)],
+                    out=mix[:, pair_tiles(pair), chunk_cols(c)],
+                    in_=x_sb[:, pair_tiles(pair), chunk_cols(c)],
                     func=ACT.Copy,
                     scale=one_minus[:, 0:1],
                 )
-            else:
-                nc.vector.tensor_scalar_mul(
-                    out=mix[:, h, chunk_cols(c)], in0=x_sb[:, h, chunk_cols(c)], scalar1=one_minus[:, 0:1]
-                )
 
-        def project(c, h):
-            y_ps = psum.tile([P, BANK], F32, tag="bank")
-            nc.tensor.matmul_mx(
-                out=y_ps[:],
-                lhsT=w_codes[:, h * P : (h + 1) * P].bitcast(FP8X4),
-                lhsT_scale=w_scales[:, h * P : (h + 1) * P],
-                rhs=a_codes[:, chunk_cols(c)].bitcast(FP8X4),
-                rhs_scale=a_scales[:, chunk_cols(c)],
-                start=True,
-                stop=True,
-            )
-            attn_g_sb = stage.tile([P, BANK], F32)
-            nc.scalar.activation(
-                out=attn_g_sb[:], in_=y_ps[:], func=ACT.Identity, bias=b_col[:, h : h + 1], scale=1.0
-            )
-            nc.sync.dma_start(out=attn_g_view[h][:, chunk_cols(c)], in_=attn_g_sb[:])
+        def project(c, pair):
+            attn_g_sb = stage.tile([P, 2, BANK], F32)
+            for i in range(2):
+                h = 2 * pair + i
+                y_ps = psum.tile([P, BANK], F32, tag="bank")
+                nc.tensor.matmul_mx(
+                    out=y_ps[:],
+                    lhsT=w_codes[:, h * P : (h + 1) * P].bitcast(FP8X4),
+                    lhsT_scale=w_scales[:, h * P : (h + 1) * P],
+                    rhs=a_codes[:, chunk_cols(c)].bitcast(FP8X4),
+                    rhs_scale=a_scales[:, chunk_cols(c)],
+                    start=True,
+                    stop=True,
+                )
+                nc.scalar.activation(
+                    out=attn_g_sb[:, i, :], in_=y_ps[:], func=ACT.Identity, bias=b_col[:, h : h + 1], scale=1.0
+                )
+            nc.sync.dma_start(out=attn_g_view[:, pair_tiles(pair), chunk_cols(c)], in_=attn_g_sb[:])
             nc.vector.scalar_tensor_tensor(
-                out=mix[:, h, chunk_cols(c)],
+                out=mix[:, pair_tiles(pair), chunk_cols(c)],
                 in0=attn_g_sb[:],
                 scalar=alpha[:, 0:1],
-                in1=mix[:, h, chunk_cols(c)],
+                in1=mix[:, pair_tiles(pair), chunk_cols(c)],
                 op0=ALU.mult,
                 op1=ALU.add,
             )
-            nc.sync.dma_start(out=out_view[h][:, chunk_cols(c)], in_=mix[:, h, chunk_cols(c)])
+            nc.sync.dma_start(
+                out=out_view[:, pair_tiles(pair), chunk_cols(c)], in_=mix[:, pair_tiles(pair), chunk_cols(c)]
+            )
 
         normalise(0)
         quantise_attn(0)
@@ -260,24 +279,25 @@ def tile_selfattention3d_pa_kernel(
             scales=w_scales[:],
             in_=w_grouped[:].rearrange("p h t -> p (h t)"),
         )
-        for h in range(0, CH_TILES, 2):
-            scale_x(0, h)
+        for pair in range(PAIRS // 2, PAIRS):
+            scale_x(0, pair)
         for nb in range(BLOCKS):
             attend(0, nb)
         normalise(1)
         quantise_a(0)
         quantise_attn(1)
-        for h in range(1, CH_TILES, 2):
-            scale_x(0, h)
+        for pair in range(PAIRS // 2):
+            scale_x(0, pair)
 
         for c in range(CHUNKS):
-            for h in range(CH_TILES):
-                project(c, h)
+            for pair in range(PAIRS):
+                project(c, pair)
                 if c + 1 < CHUNKS:
-                    scale_x(c + 1, h)
-                    if h < BLOCKS:
-                        attend(c + 1, h)
-                if h == BLOCKS - 1:
+                    scale_x(c + 1, pair)
+                    if pair < PAIRS // 2:
+                        attend(c + 1, 2 * pair)
+                        attend(c + 1, 2 * pair + 1)
+                if pair == PAIRS // 2 - 1:
                     if c + 2 < CHUNKS:
                         normalise(c + 2)
                     if c + 1 < CHUNKS:

@@ -101,6 +101,18 @@ def tile_selfattention3d_pa_kernel(
         g_grouped = keep.tile([P, PACK, P, PACK], BF16, align_bytes=64)
         nc.scalar.copy(out=g_grouped[:], in_=g_raw[:].rearrange("p j (h t) -> p t h j", t=PACK))
 
+        mix = keep.tile([P, CH_TILES, QUERIES], F32)
+        for c in range(CHUNKS):
+            for pair in range(PAIRS // 2):
+                nc.gpsimd.tensor_scalar(
+                    out=mix[:, 2 * pair : 2 * pair + 2, c * BANK : (c + 1) * BANK],
+                    in0=x_sb[:, 2 * pair : 2 * pair + 2, c * BANK : (c + 1) * BANK],
+                    scalar1=one_minus[:, 0:1],
+                    scalar2=0.0,
+                    op0=ALU.mult,
+                    op1=ALU.add,
+                )
+
         e = keep.tile([P, PACK, QUERIES], F32)
         bank_max = keep.tile([P, PACK, CHUNKS], F32)
         neg_max = keep.tile([P, PACK], F32)
@@ -172,7 +184,6 @@ def tile_selfattention3d_pa_kernel(
         attn_scales = keep.tile([P, QUERIES], U8, align_bytes=64)
         a_codes = keep.tile([P, QUERIES], U32, align_bytes=64)
         a_scales = keep.tile([P, QUERIES], U8, align_bytes=64)
-        mix = keep.tile([P, CH_TILES, QUERIES], F32)
         out_view = out_0.rearrange("b (h p) f r c -> p (b h) (f r c)", p=P)
         attn_g_view = out_1.rearrange("b (h p) f r c -> p (b h) (f r c)", p=P)
         attn_grouped = {}
@@ -228,19 +239,11 @@ def tile_selfattention3d_pa_kernel(
             return slice(2 * pair, 2 * pair + 2)
 
         def scale_x(c, pair):
-            if pair < PAIRS // 2:
-                nc.vector.tensor_scalar_mul(
-                    out=mix[:, pair_tiles(pair), chunk_cols(c)],
-                    in0=x_sb[:, pair_tiles(pair), chunk_cols(c)],
-                    scalar1=one_minus[:, 0:1],
-                )
-            else:
-                nc.scalar.activation(
-                    out=mix[:, pair_tiles(pair), chunk_cols(c)],
-                    in_=x_sb[:, pair_tiles(pair), chunk_cols(c)],
-                    func=ACT.Copy,
-                    scale=one_minus[:, 0:1],
-                )
+            nc.vector.tensor_scalar_mul(
+                out=mix[:, pair_tiles(pair), chunk_cols(c)],
+                in0=x_sb[:, pair_tiles(pair), chunk_cols(c)],
+                scalar1=one_minus[:, 0:1],
+            )
 
         def project(c, pair):
             attn_g_sb = stage.tile([P, 2, BANK], F32)
@@ -279,24 +282,23 @@ def tile_selfattention3d_pa_kernel(
             scales=w_scales[:],
             in_=w_grouped[:].rearrange("p h t -> p (h t)"),
         )
-        for pair in range(PAIRS // 2, PAIRS):
-            scale_x(0, pair)
         for nb in range(BLOCKS):
             attend(0, nb)
         normalise(1)
         quantise_a(0)
         quantise_attn(1)
-        for pair in range(PAIRS // 2):
+        for pair in range(PAIRS // 2, PAIRS):
             scale_x(0, pair)
 
         for c in range(CHUNKS):
             for pair in range(PAIRS):
                 project(c, pair)
                 if c + 1 < CHUNKS:
-                    scale_x(c + 1, pair)
                     if pair < PAIRS // 2:
                         attend(c + 1, 2 * pair)
                         attend(c + 1, 2 * pair + 1)
+                    else:
+                        scale_x(c + 1, pair)
                 if pair == PAIRS // 2 - 1:
                     if c + 2 < CHUNKS:
                         normalise(c + 2)

@@ -15,17 +15,20 @@ AX = mybir.AxisListType
 P = 128
 PACK = 4
 BANK = 512
+PSUM_BANKS = 8
 QUERIES = 2048
 KEYS = 512
 C_QK = 128
 C_V = 512
 CH = 1024
 CHUNKS = QUERIES // BANK
+UNIT = 256
+UNITS_PER_CHUNK = BANK // UNIT
+UNIT_BLOCKS = UNIT // P
 CH_TILES = CH // P
-BLOCKS = BANK // P
-PSUM_BANKS = 8
-STAGE_BUFS = 4
 PAIRS = CH_TILES // 2
+HALF = PAIRS // 2
+STAGE_BUFS = 6
 
 FLOPS = 2 * QUERIES * KEYS * C_QK + 2 * QUERIES * KEYS * C_V + 2 * CH * C_V * QUERIES
 
@@ -67,6 +70,16 @@ def tile_selfattention3d_pa_kernel(
         ident_f32 = keep.tile([P, P], F32)
         make_identity(nc, ident_f32[:])
 
+        phiT = keep.tile([P, PACK, P], BF16)
+        phiT_ps = psum.tile([P, PACK, P], BF16, tag="bank")
+        for t in range(PACK):
+            nc.tensor.transpose(phiT_ps[:, t, :], phi_sb[:, t, :], ident_bf[:])
+        nc.vector.tensor_copy(out=phiT[:], in_=phiT_ps[:])
+        bT_ps = psum.tile([P, P], BF16, tag="bank")
+        nc.tensor.transpose(bT_ps[:], b_rows[:], ident_bf[:])
+        b_col = keep.tile([P, CH_TILES], F32)
+        nc.vector.tensor_copy(out=b_col[:], in_=bT_ps[:, 0:CH_TILES])
+
         exp_neg = keep.tile([P, 1], F32)
         nc.scalar.activation(out=exp_neg[:], in_=gamma_sb[:], func=ACT.Exp, scale=-1.0)
         alpha = keep.tile([P, 1], F32)
@@ -77,65 +90,32 @@ def tile_selfattention3d_pa_kernel(
             out=one_minus[:], in0=alpha[:], scalar1=-1.0, scalar2=1.0, op0=ALU.mult, op1=ALU.add
         )
 
-        phiT = keep.tile([P, PACK, P], BF16)
-        phiT_ps = psum.tile([P, PACK, P], BF16, tag="bank")
-        for t in range(PACK):
-            nc.tensor.transpose(phiT_ps[:, t, :], phi_sb[:, t, :], ident_bf[:])
-        nc.vector.tensor_copy(out=phiT[:], in_=phiT_ps[:])
-
         thetaT = keep.tile([P, CHUNKS, PACK, P], BF16)
-        for c in range(CHUNKS):
-            thetaT_ps = psum.tile([P, PACK, P], BF16, tag="bank")
-            for j in range(PACK):
-                nc.tensor.transpose(thetaT_ps[:, j, :], theta_sb[:, c, j, :], ident_bf[:])
-            if c % 2 == 0:
-                nc.scalar.copy(out=thetaT[:, c, :, :], in_=thetaT_ps[:])
-            else:
-                nc.vector.tensor_copy(out=thetaT[:, c, :, :], in_=thetaT_ps[:])
-
-        bT_ps = psum.tile([P, P], BF16, tag="bank")
-        nc.tensor.transpose(bT_ps[:], b_rows[:], ident_bf[:])
-        b_col = keep.tile([P, CH_TILES], F32)
-        nc.vector.tensor_copy(out=b_col[:], in_=bT_ps[:, 0:CH_TILES])
-
-        g_grouped = keep.tile([P, PACK, P, PACK], BF16, align_bytes=64)
-        nc.scalar.copy(out=g_grouped[:], in_=g_raw[:].rearrange("p j (h t) -> p t h j", t=PACK))
-
-        mix = keep.tile([P, CH_TILES, QUERIES], F32)
-        for c in range(CHUNKS):
-            for pair in range(PAIRS // 2):
-                nc.gpsimd.tensor_scalar(
-                    out=mix[:, 2 * pair : 2 * pair + 2, c * BANK : (c + 1) * BANK],
-                    in0=x_sb[:, 2 * pair : 2 * pair + 2, c * BANK : (c + 1) * BANK],
-                    scalar1=one_minus[:, 0:1],
-                    scalar2=0.0,
-                    op0=ALU.mult,
-                    op1=ALU.add,
-                )
-
         e = keep.tile([P, PACK, QUERIES], F32)
         bank_max = keep.tile([P, PACK, CHUNKS], F32)
         neg_max = keep.tile([P, PACK], F32)
         key_sum = keep.tile([P, PACK], F32)
-        for t in range(PACK):
-            for c in range(CHUNKS):
-                s_ps = psum.tile([P, BANK], F32, tag="bank")
-                nc.tensor.matmul(
-                    s_ps[:],
-                    lhsT=phiT[:, t, :],
-                    rhs=thetaT[:, c, :, :].rearrange("k j p -> k (j p)"),
-                    start=True,
-                    stop=True,
-                )
-                nc.vector.tensor_scalar(
-                    out=e[:, t, c * BANK : (c + 1) * BANK],
-                    in0=s_ps[:],
-                    scalar1=1.0,
-                    scalar2=None,
-                    op0=ALU.mult,
-                    op1=ALU.max,
-                    accum_out=bank_max[:, t, c : c + 1],
-                )
+
+        def scores(t, c):
+            s_ps = psum.tile([P, BANK], F32, tag="bank")
+            nc.tensor.matmul(
+                s_ps[:],
+                lhsT=phiT[:, t, :],
+                rhs=thetaT[:, c, :, :].rearrange("k j p -> k (j p)"),
+                start=True,
+                stop=True,
+            )
+            nc.vector.tensor_scalar(
+                out=e[:, t, c * BANK : (c + 1) * BANK],
+                in0=s_ps[:],
+                scalar1=1.0,
+                scalar2=None,
+                op0=ALU.mult,
+                op1=ALU.max,
+                accum_out=bank_max[:, t, c : c + 1],
+            )
+
+        def exponentials(t):
             nc.vector.tensor_reduce(
                 out=neg_max[:, t : t + 1], in_=bank_max[:, t, :], axis=AX.X, op=ALU.max, negate=True
             )
@@ -148,6 +128,27 @@ def tile_selfattention3d_pa_kernel(
                 accum_out=key_sum[:, t : t + 1],
             )
 
+        for c in range(CHUNKS):
+            thetaT_ps = psum.tile([P, PACK, P], BF16, tag="bank")
+            for j in range(PACK):
+                nc.tensor.transpose(thetaT_ps[:, j, :], theta_sb[:, c, j, :], ident_bf[:])
+            if c < CHUNKS // 2:
+                nc.vector.tensor_copy(out=thetaT[:, c, :, :], in_=thetaT_ps[:])
+            else:
+                nc.scalar.copy(out=thetaT[:, c, :, :], in_=thetaT_ps[:])
+            if c > 0:
+                scores(0, c - 1)
+        scores(0, CHUNKS - 1)
+
+        g_grouped = keep.tile([P, PACK, P, PACK], BF16, align_bytes=64)
+        nc.scalar.copy(out=g_grouped[:], in_=g_raw[:].rearrange("p j (h t) -> p t h j", t=PACK))
+
+        exponentials(0)
+        for t in range(1, PACK):
+            for c in range(CHUNKS):
+                scores(t, c)
+            exponentials(t)
+
         g_codes = keep.tile([P, C_V], U32, align_bytes=64)
         g_scales = keep.tile([P, C_V], U8, align_bytes=64)
         nc.vector.quantize_mx(
@@ -158,13 +159,28 @@ def tile_selfattention3d_pa_kernel(
 
         w_grouped = keep.tile([P, CH, PACK], BF16, align_bytes=64)
         w_words = w_grouped[:].bitcast(F32)
-        for pair in range(PAIRS):
+        w_codes = keep.tile([P, CH], U32, align_bytes=64)
+        w_scales = keep.tile([P, CH], U8, align_bytes=64)
+
+        def transpose_w(pair):
             wT_ps = psum.tile([P, 2, 2 * P], F32, tag="bank")
             for i in range(2):
                 words = w_sb[:, 2 * pair + i, :].bitcast(F32).rearrange("p (q u) -> p u q", u=2)
                 for u in range(2):
                     nc.tensor.transpose(wT_ps[:, u, i * P : (i + 1) * P], words[:, u, :], ident_f32[:])
-            if pair < PAIRS // 2:
+            return wT_ps
+
+        def quantise_w(half):
+            rows = slice(half * (CH // 2), (half + 1) * (CH // 2))
+            nc.vector.quantize_mx(
+                out=w_codes[:, rows].bitcast(FP8X4),
+                scales=w_scales[:, rows],
+                in_=w_grouped[:, rows, :].rearrange("p h t -> p (h t)"),
+            )
+
+        for pair in range(PAIRS):
+            wT_ps = transpose_w(pair)
+            if pair < HALF:
                 nc.vector.tensor_copy(
                     out=w_words[:, 2 * pair * P : (2 * pair + 2) * P, :],
                     in_=wT_ps[:].rearrange("q u h -> q h u"),
@@ -174,8 +190,7 @@ def tile_selfattention3d_pa_kernel(
                     out=w_words[:, 2 * pair * P : (2 * pair + 2) * P, :],
                     in_=wT_ps[:].rearrange("q u h -> q h u"),
                 )
-        w_codes = keep.tile([P, CH], U32, align_bytes=64)
-        w_scales = keep.tile([P, CH], U8, align_bytes=64)
+        quantise_w(0)
 
         recip = keep.tile([P, PACK], F32)
         nc.vector.reciprocal(out=recip[:], in_=key_sum[:])
@@ -184,66 +199,76 @@ def tile_selfattention3d_pa_kernel(
         attn_scales = keep.tile([P, QUERIES], U8, align_bytes=64)
         a_codes = keep.tile([P, QUERIES], U32, align_bytes=64)
         a_scales = keep.tile([P, QUERIES], U8, align_bytes=64)
+        mix = keep.tile([P, CH_TILES, QUERIES], F32)
         out_view = out_0.rearrange("b (h p) f r c -> p (b h) (f r c)", p=P)
         attn_g_view = out_1.rearrange("b (h p) f r c -> p (b h) (f r c)", p=P)
         attn_grouped = {}
         a_grouped = {}
 
+        def unit_cols(u):
+            return slice(u * UNIT, (u + 1) * UNIT)
+
         def chunk_cols(c):
             return slice(c * BANK, (c + 1) * BANK)
-
-        def normalise(c):
-            attn_grouped[c] = work.tile([P, BANK, PACK], BF16, align_bytes=64, name="attn_grouped")
-            nc.vector.tensor_tensor(
-                out=attn_grouped[c][:],
-                in0=e[:, :, chunk_cols(c)].rearrange("p t n -> p n t"),
-                in1=recip[:].unsqueeze(1).to_broadcast([P, BANK, PACK]),
-                op=ALU.mult,
-            )
-
-        def quantise_attn(c):
-            nc.vector.quantize_mx(
-                out=attn_codes[:, chunk_cols(c)].bitcast(FP8X4),
-                scales=attn_scales[:, chunk_cols(c)],
-                in_=attn_grouped[c][:].rearrange("p n t -> p (n t)"),
-            )
-
-        def attend(c, nb):
-            if nb == 0:
-                a_grouped[c] = work.tile([P, BANK, PACK], BF16, align_bytes=64, name="a_grouped")
-            n0 = c * BANK + nb * P
-            a_ps = psum.tile([P, PACK, P], F32, tag="bank")
-            for t in range(PACK):
-                nc.tensor.matmul_mx(
-                    out=a_ps[:, t, :],
-                    lhsT=g_codes[:, t * P : (t + 1) * P].bitcast(FP8X4),
-                    lhsT_scale=g_scales[:, t * P : (t + 1) * P],
-                    rhs=attn_codes[:, n0 : n0 + P].bitcast(FP8X4),
-                    rhs_scale=attn_scales[:, n0 : n0 + P],
-                    start=True,
-                    stop=True,
-                )
-            nc.scalar.copy(
-                out=a_grouped[c][:, nb * P : (nb + 1) * P, :],
-                in_=a_ps[:].rearrange("p t n -> p n t"),
-            )
-
-        def quantise_a(c):
-            nc.vector.quantize_mx(
-                out=a_codes[:, chunk_cols(c)].bitcast(FP8X4),
-                scales=a_scales[:, chunk_cols(c)],
-                in_=a_grouped[c][:].rearrange("p n t -> p (n t)"),
-            )
 
         def pair_tiles(pair):
             return slice(2 * pair, 2 * pair + 2)
 
-        def scale_x(c, pair):
-            nc.vector.tensor_scalar_mul(
-                out=mix[:, pair_tiles(pair), chunk_cols(c)],
-                in0=x_sb[:, pair_tiles(pair), chunk_cols(c)],
-                scalar1=one_minus[:, 0:1],
+        def normalise(u):
+            attn_grouped[u] = work.tile([P, UNIT, PACK], BF16, align_bytes=64, name="attn_grouped")
+            nc.vector.tensor_tensor(
+                out=attn_grouped[u][:],
+                in0=e[:, :, unit_cols(u)].rearrange("p t n -> p n t"),
+                in1=recip[:].unsqueeze(1).to_broadcast([P, UNIT, PACK]),
+                op=ALU.mult,
             )
+            nc.vector.quantize_mx(
+                out=attn_codes[:, unit_cols(u)].bitcast(FP8X4),
+                scales=attn_scales[:, unit_cols(u)],
+                in_=attn_grouped[u][:].rearrange("p n t -> p (n t)"),
+            )
+
+        def attend(u):
+            a_grouped[u] = work.tile([P, UNIT, PACK], BF16, align_bytes=64, name="a_grouped")
+            for nb in range(UNIT_BLOCKS):
+                n0 = u * UNIT + nb * P
+                a_ps = psum.tile([P, PACK, P], F32, tag="bank")
+                for t in range(PACK):
+                    nc.tensor.matmul_mx(
+                        out=a_ps[:, t, :],
+                        lhsT=g_codes[:, t * P : (t + 1) * P].bitcast(FP8X4),
+                        lhsT_scale=g_scales[:, t * P : (t + 1) * P],
+                        rhs=attn_codes[:, n0 : n0 + P].bitcast(FP8X4),
+                        rhs_scale=attn_scales[:, n0 : n0 + P],
+                        start=True,
+                        stop=True,
+                    )
+                nc.scalar.copy(
+                    out=a_grouped[u][:, nb * P : (nb + 1) * P, :],
+                    in_=a_ps[:].rearrange("p t n -> p n t"),
+                )
+
+        def quantise_a(u):
+            nc.vector.quantize_mx(
+                out=a_codes[:, unit_cols(u)].bitcast(FP8X4),
+                scales=a_scales[:, unit_cols(u)],
+                in_=a_grouped[u][:].rearrange("p n t -> p (n t)"),
+            )
+
+        def scale_x(c, pair):
+            if pair < HALF:
+                nc.scalar.activation(
+                    out=mix[:, pair_tiles(pair), chunk_cols(c)],
+                    in_=x_sb[:, pair_tiles(pair), chunk_cols(c)],
+                    func=ACT.Copy,
+                    scale=one_minus[:, 0:1],
+                )
+            else:
+                nc.vector.tensor_scalar_mul(
+                    out=mix[:, pair_tiles(pair), chunk_cols(c)],
+                    in0=x_sb[:, pair_tiles(pair), chunk_cols(c)],
+                    scalar1=one_minus[:, 0:1],
+                )
 
         def project(c, pair):
             attn_g_sb = stage.tile([P, 2, BANK], F32)
@@ -276,33 +301,28 @@ def tile_selfattention3d_pa_kernel(
             )
 
         normalise(0)
-        quantise_attn(0)
-        nc.vector.quantize_mx(
-            out=w_codes[:].bitcast(FP8X4),
-            scales=w_scales[:],
-            in_=w_grouped[:].rearrange("p h t -> p (h t)"),
-        )
-        for nb in range(BLOCKS):
-            attend(0, nb)
         normalise(1)
+        quantise_w(1)
+        scale_x(0, 0)
+        attend(0)
+        attend(1)
+        scale_x(0, 1)
         quantise_a(0)
-        quantise_attn(1)
-        for pair in range(PAIRS // 2, PAIRS):
-            scale_x(0, pair)
+        normalise(2)
+        quantise_a(1)
+        normalise(3)
 
         for c in range(CHUNKS):
-            for pair in range(PAIRS):
-                project(c, pair)
+            for step in range(PAIRS):
+                project(c, step)
+                if step < HALF:
+                    scale_x(c, step + HALF)
                 if c + 1 < CHUNKS:
-                    if pair < PAIRS // 2:
-                        attend(c + 1, 2 * pair)
-                        attend(c + 1, 2 * pair + 1)
+                    if step < HALF:
+                        attend(UNITS_PER_CHUNK * (c + 1) + step)
                     else:
-                        scale_x(c + 1, pair)
-                if pair == PAIRS // 2 - 1:
-                    if c + 2 < CHUNKS:
-                        normalise(c + 2)
-                    if c + 1 < CHUNKS:
-                        quantise_a(c + 1)
-                    if c + 2 < CHUNKS:
-                        quantise_attn(c + 2)
+                        scale_x(c + 1, step - HALF)
+                    if 1 <= step <= HALF:
+                        quantise_a(UNITS_PER_CHUNK * (c + 1) + step - 1)
+                if c + 2 < CHUNKS and step >= HALF:
+                    normalise(UNITS_PER_CHUNK * (c + 2) + step - HALF)

@@ -42,7 +42,6 @@ def tile_selfattention3d_pa_kernel(
         work = ctx.enter_context(tc.tile_pool(name="work", bufs=2))
         stage = ctx.enter_context(tc.tile_pool(name="stage", bufs=STAGE_BUFS))
         psum = ctx.enter_context(tc.psum_pool(name="psum", bufs=PSUM_BANKS))
-        ctx.enter_context(tc.manual_schedule())
 
         phi_sb = keep.tile([P, PACK, C_QK], BF16)
         nc.sync.dma_start(out=phi_sb[:], in_=phi.rearrange("b (p t) k -> (b p) t k", t=PACK))

@@ -24,10 +24,11 @@ CH = 1024
 CHUNKS = QUERIES // BANK
 UNIT = 256
 UNITS_PER_CHUNK = BANK // UNIT
-UNIT_BLOCKS = UNIT // P
+UNIT_BANKS = UNIT // P
 CH_TILES = CH // P
 PAIRS = CH_TILES // 2
 HALF = PAIRS // 2
+WORK_BUFS = 2
 STAGE_BUFS = 6
 
 FLOPS = 2 * QUERIES * KEYS * C_QK + 2 * QUERIES * KEYS * C_V + 2 * CH * C_V * QUERIES
@@ -39,9 +40,10 @@ def tile_selfattention3d_pa_kernel(
     nc = tc.nc
     with ExitStack() as ctx:
         keep = ctx.enter_context(tc.tile_pool(name="keep", bufs=1))
-        work = ctx.enter_context(tc.tile_pool(name="work", bufs=2))
+        work = ctx.enter_context(tc.tile_pool(name="work", bufs=WORK_BUFS))
         stage = ctx.enter_context(tc.tile_pool(name="stage", bufs=STAGE_BUFS))
         psum = ctx.enter_context(tc.psum_pool(name="psum", bufs=PSUM_BANKS))
+        ctx.enter_context(tc.manual_schedule())
 
         phi_sb = keep.tile([P, PACK, C_QK], BF16)
         nc.sync.dma_start(out=phi_sb[:], in_=phi.rearrange("b (p t) k -> (b p) t k", t=PACK))
@@ -50,11 +52,11 @@ def tile_selfattention3d_pa_kernel(
         for c in range(CHUNKS):
             nc.sync.dma_start(out=theta_sb[:, c, :, :], in_=theta_view[c])
         g_raw = keep.tile([P, PACK, C_V], BF16)
-        nc.sync.dma_start(out=g_raw[:], in_=g.rearrange("b (p j) w -> (b p) j w", j=PACK))
+        nc.sync.dma_start(out=g_raw[:], in_=g.rearrange("b (p t) v -> (b p) t v", t=PACK))
         w_sb = keep.tile([P, CH_TILES, C_V], BF16)
-        nc.sync.dma_start(out=w_sb[:], in_=w_attn_g.rearrange("(h p) k -> p h k", p=P))
+        nc.sync.dma_start(out=w_sb[:], in_=w_attn_g.rearrange("(h p) v -> p h v", p=P))
         x_sb = keep.tile([P, CH_TILES, QUERIES], BF16)
-        x_view = x.rearrange("b (h p) f r c -> (b h) p (f r c)", p=P)
+        x_view = x.rearrange("b (h p) f r s -> (b h) p (f r s)", p=P)
         for h in range(CH_TILES):
             nc.sync.dma_start(out=x_sb[:, h, :], in_=x_view[h])
 
@@ -69,28 +71,17 @@ def tile_selfattention3d_pa_kernel(
         ident_f32 = keep.tile([P, P], F32)
         make_identity(nc, ident_f32[:])
 
+        exp_neg_gamma = keep.tile([P, 1], F32)
+        nc.scalar.activation(out=exp_neg_gamma[:], in_=gamma_sb[:], func=ACT.Exp, scale=-1.0)
+
         phiT = keep.tile([P, PACK, P], BF16)
         phiT_ps = psum.tile([P, PACK, P], BF16, tag="bank")
         for t in range(PACK):
             nc.tensor.transpose(phiT_ps[:, t, :], phi_sb[:, t, :], ident_bf[:])
         nc.vector.tensor_copy(out=phiT[:], in_=phiT_ps[:])
-        bT_ps = psum.tile([P, P], BF16, tag="bank")
-        nc.tensor.transpose(bT_ps[:], b_rows[:], ident_bf[:])
-        b_col = keep.tile([P, CH_TILES], F32)
-        nc.vector.tensor_copy(out=b_col[:], in_=bT_ps[:, 0:CH_TILES])
-
-        exp_neg = keep.tile([P, 1], F32)
-        nc.scalar.activation(out=exp_neg[:], in_=gamma_sb[:], func=ACT.Exp, scale=-1.0)
-        alpha = keep.tile([P, 1], F32)
-        nc.vector.tensor_scalar_add(out=alpha[:], in0=exp_neg[:], scalar1=1.0)
-        nc.vector.reciprocal(out=alpha[:], in_=alpha[:])
-        one_minus = keep.tile([P, 1], F32)
-        nc.vector.tensor_scalar(
-            out=one_minus[:], in0=alpha[:], scalar1=-1.0, scalar2=1.0, op0=ALU.mult, op1=ALU.add
-        )
 
         thetaT = keep.tile([P, CHUNKS, PACK, P], BF16)
-        e = keep.tile([P, PACK, QUERIES], F32)
+        soft = keep.tile([P, PACK, QUERIES], F32)
         bank_max = keep.tile([P, PACK, CHUNKS], F32)
         neg_max = keep.tile([P, PACK], F32)
         key_sum = keep.tile([P, PACK], F32)
@@ -105,7 +96,7 @@ def tile_selfattention3d_pa_kernel(
                 stop=True,
             )
             nc.vector.tensor_scalar(
-                out=e[:, t, c * BANK : (c + 1) * BANK],
+                out=soft[:, t, c * BANK : (c + 1) * BANK],
                 in0=s_ps[:],
                 scalar1=1.0,
                 scalar2=None,
@@ -119,8 +110,8 @@ def tile_selfattention3d_pa_kernel(
                 out=neg_max[:, t : t + 1], in_=bank_max[:, t, :], axis=AX.X, op=ALU.max, negate=True
             )
             nc.scalar.activation(
-                out=e[:, t, :],
-                in_=e[:, t, :],
+                out=soft[:, t, :],
+                in_=soft[:, t, :],
                 func=ACT.Exp,
                 bias=neg_max[:, t : t + 1],
                 scale=1.0,
@@ -140,7 +131,7 @@ def tile_selfattention3d_pa_kernel(
         scores(0, CHUNKS - 1)
 
         g_grouped = keep.tile([P, PACK, P, PACK], BF16, align_bytes=64)
-        nc.scalar.copy(out=g_grouped[:], in_=g_raw[:].rearrange("p j (h t) -> p t h j", t=PACK))
+        nc.scalar.copy(out=g_grouped[:], in_=g_raw[:].rearrange("p t (i u) -> p u i t", u=PACK))
 
         exponentials(0)
         for t in range(1, PACK):
@@ -153,43 +144,42 @@ def tile_selfattention3d_pa_kernel(
         nc.vector.quantize_mx(
             out=g_codes[:].bitcast(FP8X4),
             scales=g_scales[:],
-            in_=g_grouped[:].rearrange("p t h j -> p (t h j)"),
+            in_=g_grouped[:].rearrange("p u i t -> p (u i t)"),
         )
+
+        alpha = keep.tile([P, 1], F32)
+        nc.vector.tensor_scalar_add(out=alpha[:], in0=exp_neg_gamma[:], scalar1=1.0)
+        nc.vector.reciprocal(out=alpha[:], in_=alpha[:])
+        one_minus_alpha = keep.tile([P, 1], F32)
+        nc.vector.tensor_scalar(
+            out=one_minus_alpha[:], in0=alpha[:], scalar1=-1.0, scalar2=1.0, op0=ALU.mult, op1=ALU.add
+        )
+
+        bT_ps = psum.tile([P, P], BF16, tag="bank")
+        nc.tensor.transpose(bT_ps[:], b_rows[:], ident_bf[:])
+        b_col = keep.tile([P, CH_TILES], F32)
+        nc.vector.tensor_copy(out=b_col[:], in_=bT_ps[:, 0:CH_TILES])
 
         w_grouped = keep.tile([P, CH, PACK], BF16, align_bytes=64)
         w_words = w_grouped[:].bitcast(F32)
-        w_codes = keep.tile([P, CH], U32, align_bytes=64)
-        w_scales = keep.tile([P, CH], U8, align_bytes=64)
-
-        def transpose_w(pair):
+        for pair in range(PAIRS):
             wT_ps = psum.tile([P, 2, 2 * P], F32, tag="bank")
             for i in range(2):
-                words = w_sb[:, 2 * pair + i, :].bitcast(F32).rearrange("p (q u) -> p u q", u=2)
-                for u in range(2):
-                    nc.tensor.transpose(wT_ps[:, u, i * P : (i + 1) * P], words[:, u, :], ident_f32[:])
-            return wT_ps
-
-        def quantise_w(half):
-            rows = slice(half * (CH // 2), (half + 1) * (CH // 2))
-            nc.vector.quantize_mx(
-                out=w_codes[:, rows].bitcast(FP8X4),
-                scales=w_scales[:, rows],
-                in_=w_grouped[:, rows, :].rearrange("p h t -> p (h t)"),
-            )
-
-        for pair in range(PAIRS):
-            wT_ps = transpose_w(pair)
+                words = w_sb[:, 2 * pair + i, :].bitcast(F32).rearrange("p (q e) -> p e q", e=2)
+                for e in range(2):
+                    nc.tensor.transpose(wT_ps[:, e, i * P : (i + 1) * P], words[:, e, :], ident_f32[:])
             if pair < HALF:
                 nc.vector.tensor_copy(
                     out=w_words[:, 2 * pair * P : (2 * pair + 2) * P, :],
-                    in_=wT_ps[:].rearrange("q u h -> q h u"),
+                    in_=wT_ps[:].rearrange("q e o -> q o e"),
                 )
             else:
                 nc.scalar.copy(
                     out=w_words[:, 2 * pair * P : (2 * pair + 2) * P, :],
-                    in_=wT_ps[:].rearrange("q u h -> q h u"),
+                    in_=wT_ps[:].rearrange("q e o -> q o e"),
                 )
-        quantise_w(0)
+        w_codes = keep.tile([P, CH], U32, align_bytes=64)
+        w_scales = keep.tile([P, CH], U8, align_bytes=64)
 
         recip = keep.tile([P, PACK], F32)
         nc.vector.reciprocal(out=recip[:], in_=key_sum[:])
@@ -199,13 +189,13 @@ def tile_selfattention3d_pa_kernel(
         a_codes = keep.tile([P, QUERIES], U32, align_bytes=64)
         a_scales = keep.tile([P, QUERIES], U8, align_bytes=64)
         mix = keep.tile([P, CH_TILES, QUERIES], F32)
-        out_view = out_0.rearrange("b (h p) f r c -> p (b h) (f r c)", p=P)
-        attn_g_view = out_1.rearrange("b (h p) f r c -> p (b h) (f r c)", p=P)
+        out_view = out_0.rearrange("b (h p) f r s -> p (b h) (f r s)", p=P)
+        attn_g_view = out_1.rearrange("b (h p) f r s -> p (b h) (f r s)", p=P)
         attn_grouped = {}
         a_grouped = {}
 
-        def unit_cols(u):
-            return slice(u * UNIT, (u + 1) * UNIT)
+        def unit_cols(unit):
+            return slice(unit * UNIT, (unit + 1) * UNIT)
 
         def chunk_cols(c):
             return slice(c * BANK, (c + 1) * BANK)
@@ -213,45 +203,47 @@ def tile_selfattention3d_pa_kernel(
         def pair_tiles(pair):
             return slice(2 * pair, 2 * pair + 2)
 
-        def normalise(u):
-            attn_grouped[u] = work.tile([P, UNIT, PACK], BF16, align_bytes=64, name="attn_grouped")
+        def normalise(unit):
+            attn_grouped[unit] = work.tile([P, UNIT, PACK], BF16, align_bytes=64, name="attn_grouped")
             nc.vector.tensor_tensor(
-                out=attn_grouped[u][:],
-                in0=e[:, :, unit_cols(u)].rearrange("p t n -> p n t"),
+                out=attn_grouped[unit][:],
+                in0=soft[:, :, unit_cols(unit)].rearrange("p t n -> p n t"),
                 in1=recip[:].unsqueeze(1).to_broadcast([P, UNIT, PACK]),
                 op=ALU.mult,
             )
+
+        def quantise_attn(unit):
             nc.vector.quantize_mx(
-                out=attn_codes[:, unit_cols(u)].bitcast(FP8X4),
-                scales=attn_scales[:, unit_cols(u)],
-                in_=attn_grouped[u][:].rearrange("p n t -> p (n t)"),
+                out=attn_codes[:, unit_cols(unit)].bitcast(FP8X4),
+                scales=attn_scales[:, unit_cols(unit)],
+                in_=attn_grouped[unit][:].rearrange("p n t -> p (n t)"),
             )
 
-        def attend(u):
-            a_grouped[u] = work.tile([P, UNIT, PACK], BF16, align_bytes=64, name="a_grouped")
-            for nb in range(UNIT_BLOCKS):
-                n0 = u * UNIT + nb * P
+        def attend(unit):
+            a_grouped[unit] = work.tile([P, UNIT, PACK], BF16, align_bytes=64, name="a_grouped")
+            for nb in range(UNIT_BANKS):
+                n0 = unit * UNIT + nb * P
                 a_ps = psum.tile([P, PACK, P], F32, tag="bank")
-                for t in range(PACK):
+                for u in range(PACK):
                     nc.tensor.matmul_mx(
-                        out=a_ps[:, t, :],
-                        lhsT=g_codes[:, t * P : (t + 1) * P].bitcast(FP8X4),
-                        lhsT_scale=g_scales[:, t * P : (t + 1) * P],
+                        out=a_ps[:, u, :],
+                        lhsT=g_codes[:, u * P : (u + 1) * P].bitcast(FP8X4),
+                        lhsT_scale=g_scales[:, u * P : (u + 1) * P],
                         rhs=attn_codes[:, n0 : n0 + P].bitcast(FP8X4),
                         rhs_scale=attn_scales[:, n0 : n0 + P],
                         start=True,
                         stop=True,
                     )
                 nc.scalar.copy(
-                    out=a_grouped[u][:, nb * P : (nb + 1) * P, :],
-                    in_=a_ps[:].rearrange("p t n -> p n t"),
+                    out=a_grouped[unit][:, nb * P : (nb + 1) * P, :],
+                    in_=a_ps[:].rearrange("p u n -> p n u"),
                 )
 
-        def quantise_a(u):
+        def quantise_a(unit):
             nc.vector.quantize_mx(
-                out=a_codes[:, unit_cols(u)].bitcast(FP8X4),
-                scales=a_scales[:, unit_cols(u)],
-                in_=a_grouped[u][:].rearrange("p n t -> p (n t)"),
+                out=a_codes[:, unit_cols(unit)].bitcast(FP8X4),
+                scales=a_scales[:, unit_cols(unit)],
+                in_=a_grouped[unit][:].rearrange("p n u -> p (n u)"),
             )
 
         def scale_x(c, pair):
@@ -260,13 +252,13 @@ def tile_selfattention3d_pa_kernel(
                     out=mix[:, pair_tiles(pair), chunk_cols(c)],
                     in_=x_sb[:, pair_tiles(pair), chunk_cols(c)],
                     func=ACT.Copy,
-                    scale=one_minus[:, 0:1],
+                    scale=one_minus_alpha[:, 0:1],
                 )
             else:
                 nc.vector.tensor_scalar_mul(
                     out=mix[:, pair_tiles(pair), chunk_cols(c)],
                     in0=x_sb[:, pair_tiles(pair), chunk_cols(c)],
-                    scalar1=one_minus[:, 0:1],
+                    scalar1=one_minus_alpha[:, 0:1],
                 )
 
         def project(c, pair):
@@ -300,8 +292,14 @@ def tile_selfattention3d_pa_kernel(
             )
 
         normalise(0)
+        quantise_attn(0)
         normalise(1)
-        quantise_w(1)
+        quantise_attn(1)
+        nc.vector.quantize_mx(
+            out=w_codes[:].bitcast(FP8X4),
+            scales=w_scales[:],
+            in_=w_grouped[:].rearrange("p o u -> p (o u)"),
+        )
         scale_x(0, 0)
         attend(0)
         attend(1)
@@ -309,7 +307,9 @@ def tile_selfattention3d_pa_kernel(
         quantise_a(0)
         normalise(2)
         quantise_a(1)
+        quantise_attn(2)
         normalise(3)
+        quantise_attn(3)
 
         for c in range(CHUNKS):
             for step in range(PAIRS):
@@ -325,3 +325,4 @@ def tile_selfattention3d_pa_kernel(
                         quantise_a(UNITS_PER_CHUNK * (c + 1) + step - 1)
                 if c + 2 < CHUNKS and step >= HALF:
                     normalise(UNITS_PER_CHUNK * (c + 2) + step - HALF)
+                    quantise_attn(UNITS_PER_CHUNK * (c + 2) + step - HALF)

@@ -22,13 +22,10 @@ C_QK = 128
 C_V = 512
 CH = 1024
 CHUNKS = QUERIES // BANK
-UNIT = 256
-UNITS_PER_CHUNK = BANK // UNIT
-UNIT_BANKS = UNIT // P
+LAST = CHUNKS - 1
 CH_TILES = CH // P
 PAIRS = CH_TILES // 2
-HALF = PAIRS // 2
-WORK_BUFS = 2
+MIX_BUFS = 4
 STAGE_BUFS = 6
 
 FLOPS = 2 * QUERIES * KEYS * C_QK + 2 * QUERIES * KEYS * C_V + 2 * CH * C_V * QUERIES
@@ -40,39 +37,45 @@ def tile_selfattention3d_pa_kernel(
     nc = tc.nc
     with ExitStack() as ctx:
         keep = ctx.enter_context(tc.tile_pool(name="keep", bufs=1))
-        work = ctx.enter_context(tc.tile_pool(name="work", bufs=WORK_BUFS))
+        work = ctx.enter_context(tc.tile_pool(name="work", bufs=4))
+        mixes = ctx.enter_context(tc.tile_pool(name="mixes", bufs=MIX_BUFS))
         stage = ctx.enter_context(tc.tile_pool(name="stage", bufs=STAGE_BUFS))
         psum = ctx.enter_context(tc.psum_pool(name="psum", bufs=PSUM_BANKS))
         ctx.enter_context(tc.manual_schedule())
 
+        zero_col = keep.tile([P, 1], F32)
+        nc.vector.memset(zero_col[:], 0.0)
+        b_rows = keep.tile([P, P], BF16)
+        nc.vector.memset(b_rows[:], 0.0)
+        gamma_row = keep.tile([P, 2], BF16)
+        nc.vector.memset(gamma_row[:], 0.0)
+        ones = keep.tile([P, P], BF16)
+        nc.vector.memset(ones[:], 1.0)
+        nc.scalar.dma_start(out=gamma_row[0:1, 0:1], in_=gamma.unsqueeze(0))
+        nc.scalar.dma_start(out=b_rows[0:CH_TILES, :], in_=b_attn_g.rearrange("(h p) -> h p", p=P))
         phi_sb = keep.tile([P, PACK, C_QK], BF16)
         nc.sync.dma_start(out=phi_sb[:], in_=phi.rearrange("b (p t) k -> (b p) t k", t=PACK))
         theta_sb = keep.tile([P, CHUNKS, PACK, C_QK], BF16)
-        theta_view = theta.rearrange("b (c j p) k -> (b c) p j k", j=PACK, p=P)
+        theta_view = theta.rearrange("b (c q j) k -> (b c) q j k", j=PACK, q=P)
         for c in range(CHUNKS):
             nc.sync.dma_start(out=theta_sb[:, c, :, :], in_=theta_view[c])
         g_raw = keep.tile([P, PACK, C_V], BF16)
         nc.sync.dma_start(out=g_raw[:], in_=g.rearrange("b (p t) v -> (b p) t v", t=PACK))
-        w_sb = keep.tile([P, CH_TILES, C_V], BF16)
-        nc.sync.dma_start(out=w_sb[:], in_=w_attn_g.rearrange("(h p) v -> p h v", p=P))
         x_sb = keep.tile([P, CH_TILES, QUERIES], BF16)
         x_view = x.rearrange("b (h p) f r s -> (b h) p (f r s)", p=P)
+        w_sb = keep.tile([P, CH_TILES, C_V], BF16)
         for h in range(CH_TILES):
+            if h == CH_TILES // 2:
+                nc.sync.dma_start(out=w_sb[:], in_=w_attn_g.rearrange("(h p) v -> p h v", p=P))
             nc.sync.dma_start(out=x_sb[:, h, :], in_=x_view[h])
-
-        gamma_sb = keep.tile([P, 1], BF16)
-        nc.scalar.dma_start(out=gamma_sb[:], in_=gamma.partition_broadcast(P))
-        b_rows = keep.tile([P, P], BF16)
-        nc.vector.memset(b_rows[:], 0.0)
-        nc.scalar.dma_start(out=b_rows[0:CH_TILES, :], in_=b_attn_g.rearrange("(h p) -> h p", p=P))
 
         ident_bf = keep.tile([P, P], BF16)
         make_identity(nc, ident_bf[:])
         ident_f32 = keep.tile([P, P], F32)
         make_identity(nc, ident_f32[:])
 
-        exp_neg_gamma = keep.tile([P, 1], F32)
-        nc.scalar.activation(out=exp_neg_gamma[:], in_=gamma_sb[:], func=ACT.Exp, scale=-1.0)
+        warm = keep.tile([P, 1], F32)
+        nc.scalar.activation(out=warm[:], in_=zero_col[:], func=ACT.Exp)
 
         phiT = keep.tile([P, PACK, P], BF16)
         phiT_ps = psum.tile([P, PACK, P], BF16, tag="bank")
@@ -82,247 +85,369 @@ def tile_selfattention3d_pa_kernel(
 
         thetaT = keep.tile([P, CHUNKS, PACK, P], BF16)
         soft = keep.tile([P, PACK, QUERIES], F32)
-        bank_max = keep.tile([P, PACK, CHUNKS], F32)
-        neg_max = keep.tile([P, PACK], F32)
-        key_sum = keep.tile([P, PACK], F32)
+        neg_max = keep.tile([P, CHUNKS, PACK], F32)
+        neg_all = keep.tile([P, PACK], F32)
+        sums = keep.tile([P, CHUNKS, PACK], F32)
 
-        def scores(t, c):
-            s_ps = psum.tile([P, BANK], F32, tag="bank")
+        def transpose_theta(c):
+            thetaT_ps = psum.tile([P, PACK, P], BF16, tag="bank", name="thetaT_ps")
+            for j in range(PACK):
+                nc.tensor.transpose(thetaT_ps[:, j, :], theta_sb[:, c, j, :], ident_bf[:])
+            if c != 1:
+                nc.scalar.copy(out=thetaT[:, c, :, :], in_=thetaT_ps[:])
+            else:
+                nc.vector.tensor_copy(out=thetaT[:, c, :, :], in_=thetaT_ps[:])
+
+        score_ps = {}
+
+        def scores(c, t):
+            s_ps = psum.tile([P, BANK], F32, tag="bank", name="s_ps")
             nc.tensor.matmul(
                 s_ps[:],
                 lhsT=phiT[:, t, :],
-                rhs=thetaT[:, c, :, :].rearrange("k j p -> k (j p)"),
+                rhs=thetaT[:, c, :, :].rearrange("k j q -> k (j q)"),
                 start=True,
                 stop=True,
             )
-            nc.vector.tensor_scalar(
-                out=soft[:, t, c * BANK : (c + 1) * BANK],
-                in0=s_ps[:],
-                scalar1=1.0,
-                scalar2=None,
-                op0=ALU.mult,
-                op1=ALU.max,
-                accum_out=bank_max[:, t, c : c + 1],
-            )
-
-        def exponentials(t):
             nc.vector.tensor_reduce(
-                out=neg_max[:, t : t + 1], in_=bank_max[:, t, :], axis=AX.X, op=ALU.max, negate=True
+                out=neg_max[:, c, t : t + 1], in_=s_ps[:], axis=AX.X, op=ALU.max, negate=True
             )
+            bias = neg_max[:, c, t : t + 1]
+            if c == LAST:
+                nc.vector.tensor_reduce(
+                    out=neg_all[:, t : t + 1], in_=neg_max[:, :, t], axis=AX.X, op=ALU.min
+                )
+                bias = neg_all[:, t : t + 1]
+            score_ps[(c, t)] = (s_ps, bias)
+
+        def exponential(c, t):
+            s_ps, bias = score_ps[(c, t)]
             nc.scalar.activation(
-                out=soft[:, t, :],
-                in_=soft[:, t, :],
+                out=soft[:, t, c * BANK : (c + 1) * BANK].rearrange("p (q j) -> p q j", j=PACK),
+                in_=s_ps[:].rearrange("p (j q) -> p q j", j=PACK),
                 func=ACT.Exp,
-                bias=neg_max[:, t : t + 1],
+                bias=bias,
                 scale=1.0,
-                accum_out=key_sum[:, t : t + 1],
+                accum_out=sums[:, c, t : t + 1],
             )
 
-        for c in range(CHUNKS):
-            thetaT_ps = psum.tile([P, PACK, P], BF16, tag="bank")
-            for j in range(PACK):
-                nc.tensor.transpose(thetaT_ps[:, j, :], theta_sb[:, c, j, :], ident_bf[:])
-            if c < CHUNKS // 2:
-                nc.vector.tensor_copy(out=thetaT[:, c, :, :], in_=thetaT_ps[:])
-            else:
-                nc.scalar.copy(out=thetaT[:, c, :, :], in_=thetaT_ps[:])
-            if c > 0:
-                scores(0, c - 1)
-        scores(0, CHUNKS - 1)
-
+        transpose_theta(0)
+        transpose_theta(1)
         g_grouped = keep.tile([P, PACK, P, PACK], BF16, align_bytes=64)
-        nc.scalar.copy(out=g_grouped[:], in_=g_raw[:].rearrange("p t (i u) -> p u i t", u=PACK))
-
-        exponentials(0)
-        for t in range(1, PACK):
-            for c in range(CHUNKS):
-                scores(t, c)
-            exponentials(t)
-
+        nc.gpsimd.tensor_scalar(
+            out=g_grouped[:],
+            in0=g_raw[:].rearrange("p t (i u) -> p u i t", u=PACK),
+            scalar1=1.0,
+            scalar2=0.0,
+            op0=ALU.mult,
+            op1=ALU.add,
+        )
         g_codes = keep.tile([P, C_V], U32, align_bytes=64)
         g_scales = keep.tile([P, C_V], U8, align_bytes=64)
+
+        for t in range(PACK):
+            scores(0, t)
+            exponential(0, t)
+        transpose_theta(2)
+        gb_ps = psum.tile([P, CH_TILES + 2], F32, tag="bank")
+        nc.tensor.matmul(gb_ps[:, 0:CH_TILES], lhsT=b_rows[:], rhs=ident_bf[:, 0:CH_TILES], start=True, stop=True)
+        nc.tensor.matmul(gb_ps[:, CH_TILES:], lhsT=ones[:], rhs=gamma_row[:], start=True, stop=True)
+        gb = keep.tile([P, CH_TILES + 2], F32)
+        nc.vector.tensor_copy(out=gb[:], in_=gb_ps[:])
+        exp_neg_gamma = keep.tile([P, 1], F32)
+        nc.scalar.activation(
+            out=exp_neg_gamma[:], in_=gb[:, CH_TILES : CH_TILES + 1], func=ACT.Exp, scale=-1.0
+        )
+        scores(1, 0)
+        exponential(1, 0)
+        alpha = keep.tile([P, 1], F32)
+        nc.vector.tensor_scalar_add(out=alpha[:], in0=exp_neg_gamma[:], scalar1=1.0)
+        nc.vector.reciprocal(out=alpha[:], in_=alpha[:])
+        one_minus_alpha = keep.tile([P, 1], F32)
+        nc.gpsimd.tensor_scalar(
+            out=one_minus_alpha[:], in0=alpha[:], scalar1=-1.0, scalar2=1.0, op0=ALU.mult, op1=ALU.add
+        )
+        alpha_b = keep.tile([P, CH_TILES], F32)
+        nc.gpsimd.tensor_scalar(
+            out=alpha_b[:], in0=gb[:, 0:CH_TILES], scalar1=alpha[:, 0:1], scalar2=0.0, op0=ALU.mult, op1=ALU.add
+        )
+        for t in range(1, PACK):
+            scores(1, t)
+            exponential(1, t)
+        transpose_theta(3)
+        for t in range(PACK):
+            scores(2, t)
+            exponential(2, t)
+        for t in range(PACK):
+            scores(LAST, t)
+            if t < PACK - 1:
+                exponential(LAST, t)
+
+        rescale = keep.tile([P, LAST, PACK], F32)
+        nc.vector.tensor_tensor(
+            out=rescale[:],
+            in0=neg_all[:].unsqueeze(1).to_broadcast([P, LAST, PACK]),
+            in1=neg_max[:, 0:LAST, :],
+            op=ALU.subtract,
+        )
+        nc.scalar.activation(out=rescale[:], in_=rescale[:], func=ACT.Exp)
+        exponential(LAST, PACK - 1)
+
         nc.vector.quantize_mx(
             out=g_codes[:].bitcast(FP8X4),
             scales=g_scales[:],
             in_=g_grouped[:].rearrange("p u i t -> p (u i t)"),
         )
-
-        alpha = keep.tile([P, 1], F32)
-        nc.vector.tensor_scalar_add(out=alpha[:], in0=exp_neg_gamma[:], scalar1=1.0)
-        nc.vector.reciprocal(out=alpha[:], in_=alpha[:])
-        one_minus_alpha = keep.tile([P, 1], F32)
-        nc.vector.tensor_scalar(
-            out=one_minus_alpha[:], in0=alpha[:], scalar1=-1.0, scalar2=1.0, op0=ALU.mult, op1=ALU.add
+        scaled_sums = keep.tile([P, LAST, PACK], F32)
+        nc.vector.tensor_tensor(out=scaled_sums[:], in0=rescale[:], in1=sums[:, 0:LAST, :], op=ALU.mult)
+        key_sum = keep.tile([P, PACK], F32)
+        nc.vector.tensor_reduce(
+            out=key_sum[:], in_=scaled_sums[:].rearrange("p c t -> p t c"), axis=AX.X, op=ALU.add
         )
-
-        bT_ps = psum.tile([P, P], BF16, tag="bank")
-        nc.tensor.transpose(bT_ps[:], b_rows[:], ident_bf[:])
-        b_col = keep.tile([P, CH_TILES], F32)
-        nc.vector.tensor_copy(out=b_col[:], in_=bT_ps[:, 0:CH_TILES])
+        nc.vector.tensor_add(out=key_sum[:], in0=key_sum[:], in1=sums[:, LAST, :])
+        factor_last = keep.tile([P, PACK], F32)
+        nc.vector.reciprocal(out=factor_last[:], in_=key_sum[:])
+        factor = keep.tile([P, LAST, PACK], F32)
 
         w_grouped = keep.tile([P, CH, PACK], BF16, align_bytes=64)
         w_words = w_grouped[:].bitcast(F32)
-        for pair in range(PAIRS):
-            wT_ps = psum.tile([P, 2, 2 * P], F32, tag="bank")
+        w_codes = keep.tile([P, CH], U32, align_bytes=64)
+        w_scales = keep.tile([P, CH], U8, align_bytes=64)
+        wT = {}
+
+        def transpose_w(pair):
+            wT[pair] = psum.tile([P, 2, 2 * P], F32, tag="bank", name="wT_ps")
             for i in range(2):
                 words = w_sb[:, 2 * pair + i, :].bitcast(F32).rearrange("p (q e) -> p e q", e=2)
                 for e in range(2):
-                    nc.tensor.transpose(wT_ps[:, e, i * P : (i + 1) * P], words[:, e, :], ident_f32[:])
-            if pair < HALF:
-                nc.vector.tensor_copy(
-                    out=w_words[:, 2 * pair * P : (2 * pair + 2) * P, :],
-                    in_=wT_ps[:].rearrange("q e o -> q o e"),
-                )
-            else:
-                nc.scalar.copy(
-                    out=w_words[:, 2 * pair * P : (2 * pair + 2) * P, :],
-                    in_=wT_ps[:].rearrange("q e o -> q o e"),
-                )
-        w_codes = keep.tile([P, CH], U32, align_bytes=64)
-        w_scales = keep.tile([P, CH], U8, align_bytes=64)
+                    nc.tensor.transpose(wT[pair][:, e, i * P : (i + 1) * P], words[:, e, :], ident_f32[:])
 
-        recip = keep.tile([P, PACK], F32)
-        nc.vector.reciprocal(out=recip[:], in_=key_sum[:])
+        def copy_w(pair):
+            nc.scalar.copy(
+                out=w_words[:, 2 * pair * P : (2 * pair + 2) * P, :],
+                in_=wT[pair][:].rearrange("q e o -> q o e"),
+            )
+
+        def quantise_w(half):
+            cols = slice(half * CH // 2, (half + 1) * CH // 2)
+            nc.vector.quantize_mx(
+                out=w_codes[:, cols].bitcast(FP8X4),
+                scales=w_scales[:, cols],
+                in_=w_grouped[:, cols, :].rearrange("p o u -> p (o u)"),
+            )
 
         attn_codes = keep.tile([P, QUERIES], U32, align_bytes=64)
         attn_scales = keep.tile([P, QUERIES], U8, align_bytes=64)
         a_codes = keep.tile([P, QUERIES], U32, align_bytes=64)
         a_scales = keep.tile([P, QUERIES], U8, align_bytes=64)
-        mix = keep.tile([P, CH_TILES, QUERIES], F32)
         out_view = out_0.rearrange("b (h p) f r s -> p (b h) (f r s)", p=P)
         attn_g_view = out_1.rearrange("b (h p) f r s -> p (b h) (f r s)", p=P)
         attn_grouped = {}
         a_grouped = {}
+        mix = {}
 
-        def unit_cols(unit):
-            return slice(unit * UNIT, (unit + 1) * UNIT)
+        def scale_x(c, pair):
+            mix[(c, pair)] = mixes.tile([P, 2, BANK], F32, name="mix%d" % (order.index(c) % 2))
+            for i in range(2):
+                h = 2 * pair + i
+                nc.gpsimd.tensor_scalar(
+                    out=mix[(c, pair)][:, i, :],
+                    in0=x_sb[:, h, c * BANK : (c + 1) * BANK],
+                    scalar1=one_minus_alpha[:, 0:1],
+                    scalar2=alpha_b[:, h : h + 1],
+                    op0=ALU.mult,
+                    op1=ALU.add,
+                )
 
-        def chunk_cols(c):
-            return slice(c * BANK, (c + 1) * BANK)
-
-        def pair_tiles(pair):
-            return slice(2 * pair, 2 * pair + 2)
-
-        def normalise(unit):
-            attn_grouped[unit] = work.tile([P, UNIT, PACK], BF16, align_bytes=64, name="attn_grouped")
+        def normalise(n0, width):
+            c = n0 // BANK
+            grouped = work.tile([P, 2 * P, PACK], BF16, align_bytes=64, name="attn_grouped")
+            attn_grouped[n0] = grouped
+            fac = factor_last[:] if c == LAST else factor[:, c, :]
             nc.vector.tensor_tensor(
-                out=attn_grouped[unit][:],
-                in0=soft[:, :, unit_cols(unit)].rearrange("p t n -> p n t"),
-                in1=recip[:].unsqueeze(1).to_broadcast([P, UNIT, PACK]),
+                out=grouped[:, 0:width, :],
+                in0=soft[:, :, n0 : n0 + width].rearrange("p t n -> p n t"),
+                in1=fac.unsqueeze(1).to_broadcast([P, width, PACK]),
                 op=ALU.mult,
             )
 
-        def quantise_attn(unit):
+        def quantise_attn(n0, width):
             nc.vector.quantize_mx(
-                out=attn_codes[:, unit_cols(unit)].bitcast(FP8X4),
-                scales=attn_scales[:, unit_cols(unit)],
-                in_=attn_grouped[unit][:].rearrange("p n t -> p (n t)"),
+                out=attn_codes[:, n0 : n0 + width].bitcast(FP8X4),
+                scales=attn_scales[:, n0 : n0 + width],
+                in_=attn_grouped[n0][:, 0:width, :].rearrange("p n t -> p (n t)"),
             )
 
-        def attend(unit):
-            a_grouped[unit] = work.tile([P, UNIT, PACK], BF16, align_bytes=64, name="a_grouped")
-            for nb in range(UNIT_BANKS):
-                n0 = unit * UNIT + nb * P
-                a_ps = psum.tile([P, PACK, P], F32, tag="bank")
+        def attend(n0, width):
+            grouped = work.tile([P, 2 * P, PACK], BF16, align_bytes=64, name="a_grouped")
+            a_grouped[n0] = grouped
+            for nb in range(width // P):
+                q0 = n0 + nb * P
+                a_ps = psum.tile([P, PACK, P], F32, tag="bank", name="a_ps")
                 for u in range(PACK):
                     nc.tensor.matmul_mx(
                         out=a_ps[:, u, :],
                         lhsT=g_codes[:, u * P : (u + 1) * P].bitcast(FP8X4),
                         lhsT_scale=g_scales[:, u * P : (u + 1) * P],
-                        rhs=attn_codes[:, n0 : n0 + P].bitcast(FP8X4),
-                        rhs_scale=attn_scales[:, n0 : n0 + P],
+                        rhs=attn_codes[:, q0 : q0 + P].bitcast(FP8X4),
+                        rhs_scale=attn_scales[:, q0 : q0 + P],
                         start=True,
                         stop=True,
                     )
                 nc.scalar.copy(
-                    out=a_grouped[unit][:, nb * P : (nb + 1) * P, :],
+                    out=grouped[:, nb * P : (nb + 1) * P, :],
                     in_=a_ps[:].rearrange("p u n -> p n u"),
                 )
 
-        def quantise_a(unit):
+        def quantise_a(n0, width):
             nc.vector.quantize_mx(
-                out=a_codes[:, unit_cols(unit)].bitcast(FP8X4),
-                scales=a_scales[:, unit_cols(unit)],
-                in_=a_grouped[unit][:].rearrange("p n u -> p (n u)"),
+                out=a_codes[:, n0 : n0 + width].bitcast(FP8X4),
+                scales=a_scales[:, n0 : n0 + width],
+                in_=a_grouped[n0][:, 0:width, :].rearrange("p n u -> p (n u)"),
             )
 
-        def scale_x(c, pair):
-            if pair < HALF:
-                nc.scalar.activation(
-                    out=mix[:, pair_tiles(pair), chunk_cols(c)],
-                    in_=x_sb[:, pair_tiles(pair), chunk_cols(c)],
-                    func=ACT.Copy,
-                    scale=one_minus_alpha[:, 0:1],
+        def project(n0, width, pair):
+            c, off = divmod(n0, BANK)
+            tiles = slice(2 * pair, 2 * pair + 2)
+            cols = slice(n0, n0 + width)
+            within = slice(off, off + width)
+            attn_g_sb = stage.tile([P, 2, BANK], F32, name="attn_g_sb")
+            share = BANK // width
+            for first in range(0, 2, share):
+                y_ps = psum.tile([P, share, width], F32, tag="bank", name="y_ps")
+                for i in range(share):
+                    h = 2 * pair + first + i
+                    nc.tensor.matmul_mx(
+                        out=y_ps[:, i, :],
+                        lhsT=w_codes[:, h * P : (h + 1) * P].bitcast(FP8X4),
+                        lhsT_scale=w_scales[:, h * P : (h + 1) * P],
+                        rhs=a_codes[:, cols].bitcast(FP8X4),
+                        rhs_scale=a_scales[:, cols],
+                        start=True,
+                        stop=True,
+                    )
+                for i in reversed(range(share)):
+                    h = 2 * pair + first + i
+                    nc.scalar.activation(
+                        out=attn_g_sb[:, first + i, 0:width],
+                        in_=y_ps[:, i, :],
+                        func=ACT.Identity,
+                        bias=gb[:, h : h + 1],
+                        scale=1.0,
+                    )
+                mixed = mix[(c, pair)][:, first : first + share, within]
+                nc.vector.scalar_tensor_tensor(
+                    out=mixed, in0=y_ps[:], scalar=alpha[:, 0:1], in1=mixed, op0=ALU.mult, op1=ALU.add
                 )
-            else:
-                nc.vector.tensor_scalar_mul(
-                    out=mix[:, pair_tiles(pair), chunk_cols(c)],
-                    in0=x_sb[:, pair_tiles(pair), chunk_cols(c)],
-                    scalar1=one_minus_alpha[:, 0:1],
-                )
+            nc.sync.dma_start(out=attn_g_view[:, tiles, cols], in_=attn_g_sb[:, :, 0:width])
+            nc.sync.dma_start(out=out_view[:, tiles, cols], in_=mix[(c, pair)][:, :, within])
 
-        def project(c, pair):
-            attn_g_sb = stage.tile([P, 2, BANK], F32)
-            for i in range(2):
-                h = 2 * pair + i
-                y_ps = psum.tile([P, BANK], F32, tag="bank")
-                nc.tensor.matmul_mx(
-                    out=y_ps[:],
-                    lhsT=w_codes[:, h * P : (h + 1) * P].bitcast(FP8X4),
-                    lhsT_scale=w_scales[:, h * P : (h + 1) * P],
-                    rhs=a_codes[:, chunk_cols(c)].bitcast(FP8X4),
-                    rhs_scale=a_scales[:, chunk_cols(c)],
-                    start=True,
-                    stop=True,
-                )
-                nc.scalar.activation(
-                    out=attn_g_sb[:, i, :], in_=y_ps[:], func=ACT.Identity, bias=b_col[:, h : h + 1], scale=1.0
-                )
-            nc.sync.dma_start(out=attn_g_view[:, pair_tiles(pair), chunk_cols(c)], in_=attn_g_sb[:])
+        attn_g_tiles = {}
+
+        def project_tile(c, h):
+            pair, i = divmod(h, 2)
+            if i == 0:
+                attn_g_tiles[0] = stage.tile([P, 2, BANK], F32, name="attn_g_sb")
+            attn_g_sb = attn_g_tiles[0]
+            cols = slice(c * BANK, (c + 1) * BANK)
+            y_ps = psum.tile([P, BANK], F32, tag="bank", name="y_ps")
+            nc.tensor.matmul_mx(
+                out=y_ps[:],
+                lhsT=w_codes[:, h * P : (h + 1) * P].bitcast(FP8X4),
+                lhsT_scale=w_scales[:, h * P : (h + 1) * P],
+                rhs=a_codes[:, cols].bitcast(FP8X4),
+                rhs_scale=a_scales[:, cols],
+                start=True,
+                stop=True,
+            )
+            nc.scalar.activation(
+                out=attn_g_sb[:, i, :], in_=y_ps[:], func=ACT.Identity, bias=gb[:, h : h + 1], scale=1.0
+            )
             nc.vector.scalar_tensor_tensor(
-                out=mix[:, pair_tiles(pair), chunk_cols(c)],
-                in0=attn_g_sb[:],
+                out=mix[(c, pair)][:, i, :],
+                in0=y_ps[:],
                 scalar=alpha[:, 0:1],
-                in1=mix[:, pair_tiles(pair), chunk_cols(c)],
+                in1=mix[(c, pair)][:, i, :],
                 op0=ALU.mult,
                 op1=ALU.add,
             )
-            nc.sync.dma_start(
-                out=out_view[:, pair_tiles(pair), chunk_cols(c)], in_=mix[:, pair_tiles(pair), chunk_cols(c)]
-            )
+            if i == 1:
+                tiles = slice(2 * pair, 2 * pair + 2)
+                nc.sync.dma_start(out=attn_g_view[:, tiles, cols], in_=attn_g_sb[:])
+                nc.sync.dma_start(out=out_view[:, tiles, cols], in_=mix[(c, pair)][:])
 
-        normalise(0)
-        quantise_attn(0)
-        normalise(1)
-        quantise_attn(1)
-        nc.vector.quantize_mx(
-            out=w_codes[:].bitcast(FP8X4),
-            scales=w_scales[:],
-            in_=w_grouped[:].rearrange("p o u -> p (o u)"),
+        order = [LAST] + list(range(LAST))
+        for pair in range(PAIRS):
+            for c in order[:2]:
+                scale_x(c, pair)
+
+        UNIT = 2 * P
+        b0 = LAST * BANK
+        b1 = b0 + UNIT
+        for pair in range(PAIRS):
+            transpose_w(pair)
+        for pair in range(PAIRS):
+            copy_w(pair)
+        normalise(b0, P)
+        normalise(b0 + P, P)
+        quantise_attn(b0, P)
+        attend(b0, P)
+        quantise_attn(b0 + P, P)
+        attend(b0 + P, P)
+        quantise_w(0)
+        normalise(b1, UNIT)
+        quantise_a(b0, P)
+        quantise_a(b0 + P, P)
+        nc.vector.tensor_tensor(
+            out=factor[:],
+            in0=rescale[:],
+            in1=factor_last[:].unsqueeze(1).to_broadcast([P, LAST, PACK]),
+            op=ALU.mult,
         )
-        scale_x(0, 0)
-        attend(0)
-        attend(1)
-        scale_x(0, 1)
-        quantise_a(0)
-        normalise(2)
-        quantise_a(1)
-        quantise_attn(2)
-        normalise(3)
-        quantise_attn(3)
+        quantise_attn(b1, UNIT)
+        quantise_w(1)
+        normalise(0, UNIT)
+        project(b0, UNIT, 0)
+        attend(b1, UNIT)
+        project(b0, UNIT, 1)
+        quantise_attn(0, UNIT)
+        quantise_a(b1, UNIT)
+        project(b0, UNIT, 2)
+        normalise(UNIT, UNIT)
+        project(b0, UNIT, 3)
+        attend(0, UNIT)
+        project(b1, UNIT, 0)
+        quantise_attn(UNIT, UNIT)
+        project(b1, UNIT, 1)
+        quantise_a(0, UNIT)
+        attend(UNIT, UNIT)
+        project(b1, UNIT, 2)
+        normalise(BANK, UNIT)
+        project(b1, UNIT, 3)
+        quantise_a(UNIT, UNIT)
 
-        for c in range(CHUNKS):
-            for step in range(PAIRS):
-                project(c, step)
-                if step < HALF:
-                    scale_x(c, step + HALF)
-                if c + 1 < CHUNKS:
-                    if step < HALF:
-                        attend(UNITS_PER_CHUNK * (c + 1) + step)
-                    else:
-                        scale_x(c + 1, step - HALF)
-                    if 1 <= step <= HALF:
-                        quantise_a(UNITS_PER_CHUNK * (c + 1) + step - 1)
-                if c + 2 < CHUNKS and step >= HALF:
-                    normalise(UNITS_PER_CHUNK * (c + 2) + step - HALF)
-                    quantise_attn(UNITS_PER_CHUNK * (c + 2) + step - HALF)
+        for c in range(LAST):
+            n0 = (c + 1) * BANK
+            n1 = n0 + UNIT
+            n2 = n0 + BANK
+            more = c + 1 < LAST
+            for h in range(CH_TILES):
+                project_tile(c, h)
+                if not more:
+                    continue
+                if h == 0:
+                    quantise_attn(n0, UNIT)
+                elif h == 1:
+                    normalise(n1, UNIT)
+                elif h == 2:
+                    attend(n0, UNIT)
+                    quantise_attn(n1, UNIT)
+                elif h == 4:
+                    attend(n1, UNIT)
+                    quantise_a(n0, UNIT)
+                elif h == 6:
+                    quantise_a(n1, UNIT)
+                    if c + 2 < LAST:
+                        normalise(n2, UNIT)
+                if h % 2 == 1:
+                    scale_x(c + 1, h // 2)

@@ -22,11 +22,12 @@ C_QK = 128
 C_V = 512
 CH = 1024
 CHUNKS = QUERIES // BANK
+FRONT = [1, 2, 3, 0]
 LAST = CHUNKS - 1
 CH_TILES = CH // P
 PAIRS = CH_TILES // 2
-MIX_BUFS = 4
-STAGE_BUFS = 6
+STAGE_BUFS = 8
+MIX_BUFS = 10
 
 FLOPS = 2 * QUERIES * KEYS * C_QK + 2 * QUERIES * KEYS * C_V + 2 * CH * C_V * QUERIES
 
@@ -38,8 +39,8 @@ def tile_selfattention3d_pa_kernel(
     with ExitStack() as ctx:
         keep = ctx.enter_context(tc.tile_pool(name="keep", bufs=1))
         work = ctx.enter_context(tc.tile_pool(name="work", bufs=4))
-        mixes = ctx.enter_context(tc.tile_pool(name="mixes", bufs=MIX_BUFS))
         stage = ctx.enter_context(tc.tile_pool(name="stage", bufs=STAGE_BUFS))
+        mixes = ctx.enter_context(tc.tile_pool(name="mixes", bufs=MIX_BUFS))
         psum = ctx.enter_context(tc.psum_pool(name="psum", bufs=PSUM_BANKS))
         ctx.enter_context(tc.manual_schedule())
 
@@ -57,7 +58,7 @@ def tile_selfattention3d_pa_kernel(
         nc.sync.dma_start(out=phi_sb[:], in_=phi.rearrange("b (p t) k -> (b p) t k", t=PACK))
         theta_sb = keep.tile([P, CHUNKS, PACK, C_QK], BF16)
         theta_view = theta.rearrange("b (c q j) k -> (b c) q j k", j=PACK, q=P)
-        for c in range(CHUNKS):
+        for c in FRONT:
             nc.sync.dma_start(out=theta_sb[:, c, :, :], in_=theta_view[c])
         g_raw = keep.tile([P, PACK, C_V], BF16)
         nc.sync.dma_start(out=g_raw[:], in_=g.rearrange("b (p t) v -> (b p) t v", t=PACK))
@@ -81,54 +82,63 @@ def tile_selfattention3d_pa_kernel(
         phiT_ps = psum.tile([P, PACK, P], BF16, tag="bank")
         for t in range(PACK):
             nc.tensor.transpose(phiT_ps[:, t, :], phi_sb[:, t, :], ident_bf[:])
-        nc.vector.tensor_copy(out=phiT[:], in_=phiT_ps[:])
+        nc.vector.tensor_scalar_mul(out=phiT[:], in0=phiT_ps[:], scalar1=-1.0)
 
         thetaT = keep.tile([P, CHUNKS, PACK, P], BF16)
         soft = keep.tile([P, PACK, QUERIES], F32)
-        neg_max = keep.tile([P, CHUNKS, PACK], F32)
+        neg_max = keep.tile([P, LAST, PACK], F32)
+        neg_before = keep.tile([P, PACK], F32)
         neg_all = keep.tile([P, PACK], F32)
         sums = keep.tile([P, CHUNKS, PACK], F32)
+        clipped = keep.tile([P, PACK, BANK], BF16)
 
-        def transpose_theta(c):
+        def transpose_theta(k):
+            c = FRONT[k]
             thetaT_ps = psum.tile([P, PACK, P], BF16, tag="bank", name="thetaT_ps")
             for j in range(PACK):
                 nc.tensor.transpose(thetaT_ps[:, j, :], theta_sb[:, c, j, :], ident_bf[:])
-            if c != 1:
+            if k < 2:
                 nc.scalar.copy(out=thetaT[:, c, :, :], in_=thetaT_ps[:])
             else:
                 nc.vector.tensor_copy(out=thetaT[:, c, :, :], in_=thetaT_ps[:])
 
         score_ps = {}
 
-        def scores(c, t):
+        def scores(k, t):
             s_ps = psum.tile([P, BANK], F32, tag="bank", name="s_ps")
             nc.tensor.matmul(
                 s_ps[:],
                 lhsT=phiT[:, t, :],
-                rhs=thetaT[:, c, :, :].rearrange("k j q -> k (j q)"),
+                rhs=thetaT[:, FRONT[k], :, :].rearrange("k j q -> k (j q)"),
                 start=True,
                 stop=True,
             )
-            nc.vector.tensor_reduce(
-                out=neg_max[:, c, t : t + 1], in_=s_ps[:], axis=AX.X, op=ALU.max, negate=True
-            )
-            bias = neg_max[:, c, t : t + 1]
-            if c == LAST:
-                nc.vector.tensor_reduce(
-                    out=neg_all[:, t : t + 1], in_=neg_max[:, :, t], axis=AX.X, op=ALU.min
-                )
+            if k < LAST:
+                bias = neg_max[:, k, t : t + 1]
+                nc.vector.tensor_reduce(out=bias, in_=s_ps[:], axis=AX.X, op=ALU.min)
+            else:
                 bias = neg_all[:, t : t + 1]
-            score_ps[(c, t)] = (s_ps, bias)
+                nc.vector.tensor_scalar(
+                    out=clipped[:, t, :],
+                    in0=s_ps[:],
+                    scalar1=neg_before[:, t : t + 1],
+                    scalar2=neg_max[:, LAST - 1, t : t + 1],
+                    op0=ALU.min,
+                    op1=ALU.min,
+                    accum_out=bias,
+                )
+            score_ps[(k, t)] = (s_ps, bias)
 
-        def exponential(c, t):
-            s_ps, bias = score_ps[(c, t)]
+        def exponential(k, t):
+            s_ps, bias = score_ps[(k, t)]
+            c = FRONT[k]
             nc.scalar.activation(
                 out=soft[:, t, c * BANK : (c + 1) * BANK].rearrange("p (q j) -> p q j", j=PACK),
                 in_=s_ps[:].rearrange("p (j q) -> p q j", j=PACK),
                 func=ACT.Exp,
                 bias=bias,
-                scale=1.0,
-                accum_out=sums[:, c, t : t + 1],
+                scale=-1.0,
+                accum_out=sums[:, k, t : t + 1],
             )
 
         transpose_theta(0)
@@ -153,31 +163,31 @@ def tile_selfattention3d_pa_kernel(
         nc.tensor.matmul(gb_ps[:, 0:CH_TILES], lhsT=b_rows[:], rhs=ident_bf[:, 0:CH_TILES], start=True, stop=True)
         nc.tensor.matmul(gb_ps[:, CH_TILES:], lhsT=ones[:], rhs=gamma_row[:], start=True, stop=True)
         gb = keep.tile([P, CH_TILES + 2], F32)
-        nc.vector.tensor_copy(out=gb[:], in_=gb_ps[:])
         exp_neg_gamma = keep.tile([P, 1], F32)
-        nc.scalar.activation(
-            out=exp_neg_gamma[:], in_=gb[:, CH_TILES : CH_TILES + 1], func=ACT.Exp, scale=-1.0
-        )
-        scores(1, 0)
-        exponential(1, 0)
         alpha = keep.tile([P, 1], F32)
-        nc.vector.tensor_scalar_add(out=alpha[:], in0=exp_neg_gamma[:], scalar1=1.0)
-        nc.vector.reciprocal(out=alpha[:], in_=alpha[:])
         one_minus_alpha = keep.tile([P, 1], F32)
+        for t in range(PACK):
+            scores(1, t)
+            if t == 0:
+                nc.vector.tensor_copy(out=gb[:], in_=gb_ps[:])
+            exponential(1, t)
+            if t == 0:
+                nc.scalar.activation(
+                    out=exp_neg_gamma[:], in_=gb[:, CH_TILES : CH_TILES + 1], func=ACT.Exp, scale=-1.0
+                )
+            elif t == 2:
+                nc.vector.tensor_scalar_add(out=alpha[:], in0=exp_neg_gamma[:], scalar1=1.0)
+            elif t == 3:
+                nc.vector.reciprocal(out=alpha[:], in_=alpha[:])
         nc.gpsimd.tensor_scalar(
             out=one_minus_alpha[:], in0=alpha[:], scalar1=-1.0, scalar2=1.0, op0=ALU.mult, op1=ALU.add
         )
-        alpha_b = keep.tile([P, CH_TILES], F32)
-        nc.gpsimd.tensor_scalar(
-            out=alpha_b[:], in0=gb[:, 0:CH_TILES], scalar1=alpha[:, 0:1], scalar2=0.0, op0=ALU.mult, op1=ALU.add
-        )
-        for t in range(1, PACK):
-            scores(1, t)
-            exponential(1, t)
         transpose_theta(3)
         for t in range(PACK):
             scores(2, t)
             exponential(2, t)
+            if t == 1:
+                nc.vector.tensor_tensor(out=neg_before[:], in0=neg_max[:, 0, :], in1=neg_max[:, 1, :], op=ALU.min)
         for t in range(PACK):
             scores(LAST, t)
             if t < PACK - 1:
@@ -187,7 +197,7 @@ def tile_selfattention3d_pa_kernel(
         nc.vector.tensor_tensor(
             out=rescale[:],
             in0=neg_all[:].unsqueeze(1).to_broadcast([P, LAST, PACK]),
-            in1=neg_max[:, 0:LAST, :],
+            in1=neg_max[:],
             op=ALU.subtract,
         )
         nc.scalar.activation(out=rescale[:], in_=rescale[:], func=ACT.Exp)
@@ -205,9 +215,8 @@ def tile_selfattention3d_pa_kernel(
             out=key_sum[:], in_=scaled_sums[:].rearrange("p c t -> p t c"), axis=AX.X, op=ALU.add
         )
         nc.vector.tensor_add(out=key_sum[:], in0=key_sum[:], in1=sums[:, LAST, :])
-        factor_last = keep.tile([P, PACK], F32)
-        nc.vector.reciprocal(out=factor_last[:], in_=key_sum[:])
-        factor = keep.tile([P, LAST, PACK], F32)
+        factor = keep.tile([P, CHUNKS, PACK], F32)
+        nc.vector.reciprocal(out=factor[:, LAST, :], in_=key_sum[:])
 
         w_grouped = keep.tile([P, CH, PACK], BF16, align_bytes=64)
         w_words = w_grouped[:].bitcast(F32)
@@ -244,30 +253,15 @@ def tile_selfattention3d_pa_kernel(
         attn_g_view = out_1.rearrange("b (h p) f r s -> p (b h) (f r s)", p=P)
         attn_grouped = {}
         a_grouped = {}
-        mix = {}
-
-        def scale_x(c, pair):
-            mix[(c, pair)] = mixes.tile([P, 2, BANK], F32, name="mix%d" % (order.index(c) % 2))
-            for i in range(2):
-                h = 2 * pair + i
-                nc.gpsimd.tensor_scalar(
-                    out=mix[(c, pair)][:, i, :],
-                    in0=x_sb[:, h, c * BANK : (c + 1) * BANK],
-                    scalar1=one_minus_alpha[:, 0:1],
-                    scalar2=alpha_b[:, h : h + 1],
-                    op0=ALU.mult,
-                    op1=ALU.add,
-                )
 
         def normalise(n0, width):
-            c = n0 // BANK
+            k = FRONT.index(n0 // BANK)
             grouped = work.tile([P, 2 * P, PACK], BF16, align_bytes=64, name="attn_grouped")
             attn_grouped[n0] = grouped
-            fac = factor_last[:] if c == LAST else factor[:, c, :]
             nc.vector.tensor_tensor(
                 out=grouped[:, 0:width, :],
                 in0=soft[:, :, n0 : n0 + width].rearrange("p t n -> p n t"),
-                in1=fac.unsqueeze(1).to_broadcast([P, width, PACK]),
+                in1=factor[:, k, :].unsqueeze(1).to_broadcast([P, width, PACK]),
                 op=ALU.mult,
             )
 
@@ -306,148 +300,143 @@ def tile_selfattention3d_pa_kernel(
                 in_=a_grouped[n0][:, 0:width, :].rearrange("p n u -> p (n u)"),
             )
 
-        def project(n0, width, pair):
-            c, off = divmod(n0, BANK)
-            tiles = slice(2 * pair, 2 * pair + 2)
-            cols = slice(n0, n0 + width)
-            within = slice(off, off + width)
-            attn_g_sb = stage.tile([P, 2, BANK], F32, name="attn_g_sb")
-            share = BANK // width
-            for first in range(0, 2, share):
-                y_ps = psum.tile([P, share, width], F32, tag="bank", name="y_ps")
-                for i in range(share):
-                    h = 2 * pair + first + i
-                    nc.tensor.matmul_mx(
-                        out=y_ps[:, i, :],
-                        lhsT=w_codes[:, h * P : (h + 1) * P].bitcast(FP8X4),
-                        lhsT_scale=w_scales[:, h * P : (h + 1) * P],
-                        rhs=a_codes[:, cols].bitcast(FP8X4),
-                        rhs_scale=a_scales[:, cols],
-                        start=True,
-                        stop=True,
-                    )
-                for i in reversed(range(share)):
-                    h = 2 * pair + first + i
-                    nc.scalar.activation(
-                        out=attn_g_sb[:, first + i, 0:width],
-                        in_=y_ps[:, i, :],
-                        func=ACT.Identity,
-                        bias=gb[:, h : h + 1],
-                        scale=1.0,
-                    )
-                mixed = mix[(c, pair)][:, first : first + share, within]
-                nc.vector.scalar_tensor_tensor(
-                    out=mixed, in0=y_ps[:], scalar=alpha[:, 0:1], in1=mixed, op0=ALU.mult, op1=ALU.add
+        mix_tile = {}
+        attn_g_tile = {}
+
+        def buffer(pool, views, n0, width, h):
+            if (n0, h) not in views:
+                tile = pool.tile([P, 2 * BANK], F32, name="%s_buffer" % ("mix" if pool is mixes else "attn_g"))
+                for i in range(2 * BANK // width):
+                    views[(n0, h + i)] = tile[:, i * width : (i + 1) * width]
+            return views[(n0, h)]
+
+        def scale_x(n0, width, h, engine):
+            out = buffer(mixes, mix_tile, n0, width, h)
+            in_ = x_sb[:, h, n0 : n0 + width]
+            if engine == "scalar":
+                nc.scalar.activation(out=out, in_=in_, func=ACT.Copy, scale=one_minus_alpha[:, 0:1])
+            elif engine == "vector":
+                nc.vector.tensor_scalar_mul(out=out, in0=in_, scalar1=one_minus_alpha[:, 0:1])
+            else:
+                nc.gpsimd.tensor_scalar(
+                    out=out, in0=in_, scalar1=one_minus_alpha[:, 0:1], scalar2=0.0, op0=ALU.mult, op1=ALU.add
                 )
-            nc.sync.dma_start(out=attn_g_view[:, tiles, cols], in_=attn_g_sb[:, :, 0:width])
-            nc.sync.dma_start(out=out_view[:, tiles, cols], in_=mix[(c, pair)][:, :, within])
 
-        attn_g_tiles = {}
+        def project(n0, width, h):
+            attn_g_sb = buffer(stage, attn_g_tile, n0, width, h)
+            for m0 in range(n0, n0 + width, BANK):
+                y_ps = psum.tile([P, BANK], F32, tag="bank", name="y_ps")
+                nc.tensor.matmul_mx(
+                    out=y_ps[:],
+                    lhsT=w_codes[:, h * P : (h + 1) * P].bitcast(FP8X4),
+                    lhsT_scale=w_scales[:, h * P : (h + 1) * P],
+                    rhs=a_codes[:, m0 : m0 + BANK].bitcast(FP8X4),
+                    rhs_scale=a_scales[:, m0 : m0 + BANK],
+                    start=True,
+                    stop=True,
+                )
+                nc.scalar.activation(
+                    out=attn_g_sb[:, m0 - n0 : m0 - n0 + BANK],
+                    in_=y_ps[:],
+                    func=ACT.Identity,
+                    bias=gb[:, h : h + 1],
+                    scale=1.0,
+                )
+            nc.sync.dma_start(out=attn_g_view[:, h, n0 : n0 + width], in_=attn_g_sb)
 
-        def project_tile(c, h):
-            pair, i = divmod(h, 2)
-            if i == 0:
-                attn_g_tiles[0] = stage.tile([P, 2, BANK], F32, name="attn_g_sb")
-            attn_g_sb = attn_g_tiles[0]
-            cols = slice(c * BANK, (c + 1) * BANK)
-            y_ps = psum.tile([P, BANK], F32, tag="bank", name="y_ps")
-            nc.tensor.matmul_mx(
-                out=y_ps[:],
-                lhsT=w_codes[:, h * P : (h + 1) * P].bitcast(FP8X4),
-                lhsT_scale=w_scales[:, h * P : (h + 1) * P],
-                rhs=a_codes[:, cols].bitcast(FP8X4),
-                rhs_scale=a_scales[:, cols],
-                start=True,
-                stop=True,
-            )
-            nc.scalar.activation(
-                out=attn_g_sb[:, i, :], in_=y_ps[:], func=ACT.Identity, bias=gb[:, h : h + 1], scale=1.0
-            )
+        def gate(n0, width, h):
+            mixed = mix_tile[(n0, h)]
             nc.vector.scalar_tensor_tensor(
-                out=mix[(c, pair)][:, i, :],
-                in0=y_ps[:],
+                out=mixed,
+                in0=attn_g_tile[(n0, h)],
                 scalar=alpha[:, 0:1],
-                in1=mix[(c, pair)][:, i, :],
+                in1=mixed,
                 op0=ALU.mult,
                 op1=ALU.add,
             )
-            if i == 1:
-                tiles = slice(2 * pair, 2 * pair + 2)
-                nc.sync.dma_start(out=attn_g_view[:, tiles, cols], in_=attn_g_sb[:])
-                nc.sync.dma_start(out=out_view[:, tiles, cols], in_=mix[(c, pair)][:])
-
-        order = [LAST] + list(range(LAST))
-        for pair in range(PAIRS):
-            for c in order[:2]:
-                scale_x(c, pair)
+            nc.sync.dma_start(out=out_view[:, h, n0 : n0 + width], in_=mixed)
 
         UNIT = 2 * P
-        b0 = LAST * BANK
-        b1 = b0 + UNIT
+        for h in range(4):
+            scale_x(0, BANK, h, "gpsimd")
         for pair in range(PAIRS):
             transpose_w(pair)
         for pair in range(PAIRS):
             copy_w(pair)
-        normalise(b0, P)
-        normalise(b0 + P, P)
-        quantise_attn(b0, P)
-        attend(b0, P)
-        quantise_attn(b0 + P, P)
-        attend(b0 + P, P)
+        for i in range(4):
+            normalise(i * P, P)
+            if i >= 1:
+                quantise_attn((i - 1) * P, P)
+                attend((i - 1) * P, P)
+            if i >= 3:
+                quantise_a((i - 3) * P, P)
+        quantise_attn(3 * P, P)
+        attend(3 * P, P)
         quantise_w(0)
-        normalise(b1, UNIT)
-        quantise_a(b0, P)
-        quantise_a(b0 + P, P)
+        quantise_a(P, P)
         nc.vector.tensor_tensor(
-            out=factor[:],
+            out=factor[:, 0:LAST, :],
             in0=rescale[:],
-            in1=factor_last[:].unsqueeze(1).to_broadcast([P, LAST, PACK]),
+            in1=factor[:, LAST, :].unsqueeze(1).to_broadcast([P, LAST, PACK]),
             op=ALU.mult,
         )
-        quantise_attn(b1, UNIT)
-        quantise_w(1)
-        normalise(0, UNIT)
-        project(b0, UNIT, 0)
-        attend(b1, UNIT)
-        project(b0, UNIT, 1)
-        quantise_attn(0, UNIT)
-        quantise_a(b1, UNIT)
-        project(b0, UNIT, 2)
-        normalise(UNIT, UNIT)
-        project(b0, UNIT, 3)
-        attend(0, UNIT)
-        project(b1, UNIT, 0)
-        quantise_attn(UNIT, UNIT)
-        project(b1, UNIT, 1)
-        quantise_a(0, UNIT)
-        attend(UNIT, UNIT)
-        project(b1, UNIT, 2)
-        normalise(BANK, UNIT)
-        project(b1, UNIT, 3)
-        quantise_a(UNIT, UNIT)
+        quantise_a(2 * P, P)
+        quantise_a(3 * P, P)
 
-        for c in range(LAST):
-            n0 = (c + 1) * BANK
-            n1 = n0 + UNIT
-            n2 = n0 + BANK
-            more = c + 1 < LAST
-            for h in range(CH_TILES):
-                project_tile(c, h)
-                if not more:
-                    continue
-                if h == 0:
-                    quantise_attn(n0, UNIT)
-                elif h == 1:
-                    normalise(n1, UNIT)
-                elif h == 2:
-                    attend(n0, UNIT)
-                    quantise_attn(n1, UNIT)
-                elif h == 4:
-                    attend(n1, UNIT)
-                    quantise_a(n0, UNIT)
-                elif h == 6:
-                    quantise_a(n1, UNIT)
-                    if c + 2 < LAST:
-                        normalise(n2, UNIT)
-                if h % 2 == 1:
-                    scale_x(c + 1, h // 2)
+        def prepare(n0):
+            normalise(n0, UNIT)
+            normalise(n0 + UNIT, UNIT)
+            quantise_attn(n0, UNIT)
+            quantise_attn(n0 + UNIT, UNIT)
+
+        quantise_w(1)
+        prepare(BANK)
+        for h in range(CH_TILES):
+            project(0, BANK, h)
+        scale_x(0, BANK, 4, "vector")
+        scale_x(0, BANK, 5, "vector")
+        scale_x(0, BANK, 6, "vector")
+        scale_x(0, BANK, 7, "vector")
+        attend(BANK, UNIT)
+        attend(BANK + UNIT, UNIT)
+        for h in range(CH_TILES):
+            gate(0, BANK, h)
+            if h == 4:
+                quantise_a(BANK, UNIT)
+            if h == 6:
+                quantise_a(BANK + UNIT, UNIT)
+        prepare(2 * BANK)
+        for h in range(CH_TILES):
+            project(BANK, BANK, h)
+            if h == 5:
+                scale_x(BANK, BANK, 0, "scalar")
+                scale_x(BANK, BANK, 1, "scalar")
+            if h == 7:
+                scale_x(BANK, BANK, 2, "scalar")
+                scale_x(BANK, BANK, 3, "scalar")
+        attend(2 * BANK, UNIT)
+        attend(2 * BANK + UNIT, UNIT)
+        prepare(3 * BANK)
+        scale_x(BANK, BANK, 4, "vector")
+        scale_x(BANK, BANK, 5, "vector")
+        attend(3 * BANK, UNIT)
+        attend(3 * BANK + UNIT, UNIT)
+        for h in range(CH_TILES):
+            gate(BANK, BANK, h)
+            if h == 1:
+                quantise_a(2 * BANK, UNIT)
+            if h == 2:
+                scale_x(BANK, BANK, 6, "vector")
+                scale_x(BANK, BANK, 7, "vector")
+                quantise_a(2 * BANK + UNIT, UNIT)
+            if h == 3:
+                quantise_a(3 * BANK, UNIT)
+            if h == 5:
+                quantise_a(3 * BANK + UNIT, UNIT)
+        scale_x(2 * BANK, 2 * BANK, 0, "vector")
+        scale_x(2 * BANK, 2 * BANK, 1, "vector")
+        for h in range(CH_TILES):
+            project(2 * BANK, 2 * BANK, h)
+            if h + 2 < CH_TILES:
+                scale_x(2 * BANK, 2 * BANK, h + 2, "vector" if h % 2 else "scalar")
+            gate(2 * BANK, 2 * BANK, h)

@@ -52,6 +52,8 @@ def tile_selfattention3d_pa_kernel(
         nc.vector.memset(gamma_row[:], 0.0)
         ones = keep.tile([P, P], BF16)
         nc.vector.memset(ones[:], 1.0)
+        busy = keep.tile([P, BANK], BF16)
+        nc.vector.memset(busy[:], 1.0)
         nc.scalar.dma_start(out=gamma_row[0:1, 0:1], in_=gamma.unsqueeze(0))
         nc.scalar.dma_start(out=b_rows[0:CH_TILES, :], in_=b_attn_g.rearrange("(h p) -> h p", p=P))
         phi_sb = keep.tile([P, PACK, C_QK], BF16)
@@ -77,6 +79,13 @@ def tile_selfattention3d_pa_kernel(
 
         warm = keep.tile([P, 1], F32)
         nc.scalar.activation(out=warm[:], in_=zero_col[:], func=ACT.Exp)
+
+        def keep_busy(rhs, times):
+            busy_ps = psum.tile([P, BANK], F32, tag="bank", name="busy_ps")
+            for turn in range(times):
+                nc.tensor.matmul(busy_ps[:], lhsT=ones[:], rhs=rhs, start=True, stop=True)
+
+        keep_busy(busy[:], 4)
 
         phiT = keep.tile([P, PACK, P], BF16)
         phiT_ps = psum.tile([P, PACK, P], BF16, tag="bank")
@@ -363,6 +372,7 @@ def tile_selfattention3d_pa_kernel(
             transpose_w(pair)
         for pair in range(PAIRS):
             copy_w(pair)
+        keep_busy(clipped[:, PACK - 1, :], 5)
         for i in range(4):
             normalise(i * P, P)
             if i >= 1:
@@ -393,12 +403,12 @@ def tile_selfattention3d_pa_kernel(
         prepare(BANK)
         for h in range(CH_TILES):
             project(0, BANK, h)
-        scale_x(0, BANK, 4, "vector")
-        scale_x(0, BANK, 5, "vector")
-        scale_x(0, BANK, 6, "vector")
-        scale_x(0, BANK, 7, "vector")
+        for h in range(4, CH_TILES):
+            scale_x(0, BANK, h, "vector")
         attend(BANK, UNIT)
         attend(BANK + UNIT, UNIT)
+        for h in range(4):
+            scale_x(BANK, BANK, h, "scalar")
         for h in range(CH_TILES):
             gate(0, BANK, h)
             if h == 4:
@@ -408,35 +418,24 @@ def tile_selfattention3d_pa_kernel(
         prepare(2 * BANK)
         for h in range(CH_TILES):
             project(BANK, BANK, h)
-            if h == 5:
-                scale_x(BANK, BANK, 0, "scalar")
-                scale_x(BANK, BANK, 1, "scalar")
-            if h == 7:
-                scale_x(BANK, BANK, 2, "scalar")
-                scale_x(BANK, BANK, 3, "scalar")
         attend(2 * BANK, UNIT)
         attend(2 * BANK + UNIT, UNIT)
         prepare(3 * BANK)
-        scale_x(BANK, BANK, 4, "vector")
-        scale_x(BANK, BANK, 5, "vector")
         attend(3 * BANK, UNIT)
         attend(3 * BANK + UNIT, UNIT)
         for h in range(CH_TILES):
             gate(BANK, BANK, h)
-            if h == 1:
+            if h < 4:
+                scale_x(BANK, BANK, h + 4, "vector")
+            if h == 4:
                 quantise_a(2 * BANK, UNIT)
-            if h == 2:
-                scale_x(BANK, BANK, 6, "vector")
-                scale_x(BANK, BANK, 7, "vector")
                 quantise_a(2 * BANK + UNIT, UNIT)
-            if h == 3:
+            if h == 6:
                 quantise_a(3 * BANK, UNIT)
-            if h == 5:
                 quantise_a(3 * BANK + UNIT, UNIT)
-        scale_x(2 * BANK, 2 * BANK, 0, "vector")
-        scale_x(2 * BANK, 2 * BANK, 1, "vector")
+        scale_x(2 * BANK, 2 * BANK, 0, "scalar")
         for h in range(CH_TILES):
             project(2 * BANK, 2 * BANK, h)
-            if h + 2 < CH_TILES:
-                scale_x(2 * BANK, 2 * BANK, h + 2, "vector" if h % 2 else "scalar")
+            if h + 1 < CH_TILES:
+                scale_x(2 * BANK, 2 * BANK, h + 1, "vector" if h % 2 else "scalar")
             gate(2 * BANK, 2 * BANK, h)

@@ -44,16 +44,14 @@ def tile_selfattention3d_pa_kernel(
         psum = ctx.enter_context(tc.psum_pool(name="psum", bufs=PSUM_BANKS))
         ctx.enter_context(tc.manual_schedule())
 
+        ones = keep.tile([P, P], BF16)
+        nc.vector.memset(ones[:], 1.0)
         zero_col = keep.tile([P, 1], F32)
         nc.vector.memset(zero_col[:], 0.0)
         b_rows = keep.tile([P, P], BF16)
         nc.vector.memset(b_rows[:], 0.0)
         gamma_row = keep.tile([P, 2], BF16)
         nc.vector.memset(gamma_row[:], 0.0)
-        ones = keep.tile([P, P], BF16)
-        nc.vector.memset(ones[:], 1.0)
-        busy = keep.tile([P, BANK], BF16)
-        nc.vector.memset(busy[:], 1.0)
         nc.scalar.dma_start(out=gamma_row[0:1, 0:1], in_=gamma.unsqueeze(0))
         nc.scalar.dma_start(out=b_rows[0:CH_TILES, :], in_=b_attn_g.rearrange("(h p) -> h p", p=P))
         phi_sb = keep.tile([P, PACK, C_QK], BF16)
@@ -85,7 +83,7 @@ def tile_selfattention3d_pa_kernel(
             for turn in range(times):
                 nc.tensor.matmul(busy_ps[:], lhsT=ones[:], rhs=rhs, start=True, stop=True)
 
-        keep_busy(busy[:], 4)
+        keep_busy(ones[:].unsqueeze(1).to_broadcast([P, PACK, P]), 3)
 
         phiT = keep.tile([P, PACK, P], BF16)
         phiT_ps = psum.tile([P, PACK, P], BF16, tag="bank")
@@ -315,8 +313,9 @@ def tile_selfattention3d_pa_kernel(
         def buffer(pool, views, n0, width, h):
             if (n0, h) not in views:
                 tile = pool.tile([P, 2 * BANK], F32, name="%s_buffer" % ("mix" if pool is mixes else "attn_g"))
-                for i in range(2 * BANK // width):
-                    views[(n0, h + i)] = tile[:, i * width : (i + 1) * width]
+                share = 2 * BANK // width
+                for i in range(share):
+                    views[(n0, h - h % share + i)] = tile[:, i * width : (i + 1) * width]
             return views[(n0, h)]
 
         def scale_x(n0, width, h, engine):
@@ -353,6 +352,28 @@ def tile_selfattention3d_pa_kernel(
                 )
             nc.sync.dma_start(out=attn_g_view[:, h, n0 : n0 + width], in_=attn_g_sb)
 
+        def project_half(n0, pair, half):
+            m0 = n0 + half * 2 * P
+            y_ps = psum.tile([P, 2, 2 * P], F32, tag="bank", name="y_ps")
+            for i in range(2):
+                h = 2 * pair + i
+                nc.tensor.matmul_mx(
+                    out=y_ps[:, i, :],
+                    lhsT=w_codes[:, h * P : (h + 1) * P].bitcast(FP8X4),
+                    lhsT_scale=w_scales[:, h * P : (h + 1) * P],
+                    rhs=a_codes[:, m0 : m0 + 2 * P].bitcast(FP8X4),
+                    rhs_scale=a_scales[:, m0 : m0 + 2 * P],
+                    start=True,
+                    stop=True,
+                )
+            for i in reversed(range(2)):
+                h = 2 * pair + i
+                piece = buffer(stage, attn_g_tile, n0, BANK, 2 * pair + i)[:, half * 2 * P : (half + 1) * 2 * P]
+                nc.scalar.activation(
+                    out=piece, in_=y_ps[:, i, :], func=ACT.Identity, bias=gb[:, h : h + 1], scale=1.0
+                )
+                nc.sync.dma_start(out=attn_g_view[:, h, m0 : m0 + 2 * P], in_=piece)
+
         def gate(n0, width, h):
             mixed = mix_tile[(n0, h)]
             nc.vector.scalar_tensor_tensor(
@@ -366,7 +387,7 @@ def tile_selfattention3d_pa_kernel(
             nc.sync.dma_start(out=out_view[:, h, n0 : n0 + width], in_=mixed)
 
         UNIT = 2 * P
-        for h in range(4):
+        for h in range(CH_TILES):
             scale_x(0, BANK, h, "gpsimd")
         for pair in range(PAIRS):
             transpose_w(pair)
@@ -384,6 +405,8 @@ def tile_selfattention3d_pa_kernel(
         attend(3 * P, P)
         quantise_w(0)
         quantise_a(P, P)
+        for pair in range(2):
+            project_half(0, pair, 0)
         nc.vector.tensor_tensor(
             out=factor[:, 0:LAST, :],
             in0=rescale[:],
@@ -401,10 +424,10 @@ def tile_selfattention3d_pa_kernel(
 
         quantise_w(1)
         prepare(BANK)
-        for h in range(CH_TILES):
-            project(0, BANK, h)
+        for pair in range(2):
+            project_half(0, pair, 1)
         for h in range(4, CH_TILES):
-            scale_x(0, BANK, h, "vector")
+            project(0, BANK, h)
         attend(BANK, UNIT)
         attend(BANK + UNIT, UNIT)
         for h in range(4):
@@ -427,13 +450,13 @@ def tile_selfattention3d_pa_kernel(
             gate(BANK, BANK, h)
             if h < 4:
                 scale_x(BANK, BANK, h + 4, "vector")
-            if h == 4:
+            if h == 2:
                 quantise_a(2 * BANK, UNIT)
                 quantise_a(2 * BANK + UNIT, UNIT)
-            if h == 6:
+            if h == 4:
                 quantise_a(3 * BANK, UNIT)
                 quantise_a(3 * BANK + UNIT, UNIT)
-        scale_x(2 * BANK, 2 * BANK, 0, "scalar")
+        scale_x(2 * BANK, 2 * BANK, 0, "vector")
         for h in range(CH_TILES):
             project(2 * BANK, 2 * BANK, h)
             if h + 1 < CH_TILES:

@@ -387,13 +387,15 @@ def tile_selfattention3d_pa_kernel(
             nc.sync.dma_start(out=out_view[:, h, n0 : n0 + width], in_=mixed)
 
         UNIT = 2 * P
-        for h in range(CH_TILES):
+        for h in range(5):
             scale_x(0, BANK, h, "gpsimd")
         for pair in range(PAIRS):
             transpose_w(pair)
         for pair in range(PAIRS):
             copy_w(pair)
         keep_busy(clipped[:, PACK - 1, :], 5)
+        for h in range(5, 6):
+            scale_x(0, BANK, h, "scalar")
         for i in range(4):
             normalise(i * P, P)
             if i >= 1:
@@ -430,8 +432,10 @@ def tile_selfattention3d_pa_kernel(
             project(0, BANK, h)
         attend(BANK, UNIT)
         attend(BANK + UNIT, UNIT)
-        for h in range(4):
+        for h in range(6):
             scale_x(BANK, BANK, h, "scalar")
+        for h in range(6, CH_TILES):
+            scale_x(0, BANK, h, "vector")
         for h in range(CH_TILES):
             gate(0, BANK, h)
             if h == 4:
@@ -448,12 +452,12 @@ def tile_selfattention3d_pa_kernel(
         attend(3 * BANK + UNIT, UNIT)
         for h in range(CH_TILES):
             gate(BANK, BANK, h)
-            if h < 4:
-                scale_x(BANK, BANK, h + 4, "vector")
-            if h == 2:
+            if h + 6 < CH_TILES:
+                scale_x(BANK, BANK, h + 6, "vector")
+            if h == 3:
                 quantise_a(2 * BANK, UNIT)
                 quantise_a(2 * BANK + UNIT, UNIT)
-            if h == 4:
+            if h == 5:
                 quantise_a(3 * BANK, UNIT)
                 quantise_a(3 * BANK + UNIT, UNIT)
         scale_x(2 * BANK, 2 * BANK, 0, "vector")

@@ -104,7 +104,7 @@ def tile_selfattention3d_pa_kernel(
             thetaT_ps = psum.tile([P, PACK, P], BF16, tag="bank", name="thetaT_ps")
             for j in range(PACK):
                 nc.tensor.transpose(thetaT_ps[:, j, :], theta_sb[:, c, j, :], ident_bf[:])
-            if k < 2:
+            if k < 3:
                 nc.scalar.copy(out=thetaT[:, c, :, :], in_=thetaT_ps[:])
             else:
                 nc.vector.tensor_copy(out=thetaT[:, c, :, :], in_=thetaT_ps[:])
@@ -164,8 +164,9 @@ def tile_selfattention3d_pa_kernel(
 
         for t in range(PACK):
             scores(0, t)
+            if t == 0:
+                transpose_theta(2)
             exponential(0, t)
-        transpose_theta(2)
         gb_ps = psum.tile([P, CH_TILES + 2], F32, tag="bank")
         nc.tensor.matmul(gb_ps[:, 0:CH_TILES], lhsT=b_rows[:], rhs=ident_bf[:, 0:CH_TILES], start=True, stop=True)
         nc.tensor.matmul(gb_ps[:, CH_TILES:], lhsT=ones[:], rhs=gamma_row[:], start=True, stop=True)

from contextlib import ExitStack

import concourse.mybir as mybir
from concourse.masks import make_identity

F32 = mybir.dt.float32
BF16 = mybir.dt.bfloat16
U32 = mybir.dt.uint32
U8 = mybir.dt.uint8
FP8X4 = mybir.dt.float8_e4m3fn_x4
ACT = mybir.ActivationFunctionType
ALU = mybir.AluOpType
AX = mybir.AxisListType

P = 128
PACK = 4
BANK = 512
PSUM_BANKS = 8
QUERIES = 2048
KEYS = 512
C_QK = 128
C_V = 512
CH = 1024
CHUNKS = QUERIES // BANK
FRONT = [1, 2, 3, 0]
LAST = CHUNKS - 1
CH_TILES = CH // P
PAIRS = CH_TILES // 2
STAGE_BUFS = 8
MIX_BUFS = 10

FLOPS = 2 * QUERIES * KEYS * C_QK + 2 * QUERIES * KEYS * C_V + 2 * CH * C_V * QUERIES


def tile_selfattention3d_pa_kernel(
    tc, theta, phi, g, x, w_attn_g, b_attn_g, gamma, out_0, out_1
):
    nc = tc.nc
    with ExitStack() as ctx:
        keep = ctx.enter_context(tc.tile_pool(name="keep", bufs=1))
        work = ctx.enter_context(tc.tile_pool(name="work", bufs=4))
        stage = ctx.enter_context(tc.tile_pool(name="stage", bufs=STAGE_BUFS))
        mixes = ctx.enter_context(tc.tile_pool(name="mixes", bufs=MIX_BUFS))
        psum = ctx.enter_context(tc.psum_pool(name="psum", bufs=PSUM_BANKS))
        ctx.enter_context(tc.manual_schedule())

        ones = keep.tile([P, P], BF16)
        nc.vector.memset(ones[:], 1.0)
        zero_col = keep.tile([P, 1], F32)
        nc.vector.memset(zero_col[:], 0.0)
        b_rows = keep.tile([P, P], BF16)
        nc.vector.memset(b_rows[:], 0.0)
        gamma_row = keep.tile([P, 2], BF16)
        nc.vector.memset(gamma_row[:], 0.0)
        nc.scalar.dma_start(out=gamma_row[0:1, 0:1], in_=gamma.unsqueeze(0))
        nc.scalar.dma_start(out=b_rows[0:CH_TILES, :], in_=b_attn_g.rearrange("(h p) -> h p", p=P))
        phi_sb = keep.tile([P, PACK, C_QK], BF16)
        nc.sync.dma_start(out=phi_sb[:], in_=phi.rearrange("b (p t) k -> (b p) t k", t=PACK))
        theta_sb = keep.tile([P, CHUNKS, PACK, C_QK], BF16)
        theta_view = theta.rearrange("b (c q j) k -> (b c) q j k", j=PACK, q=P)
        for c in FRONT:
            nc.sync.dma_start(out=theta_sb[:, c, :, :], in_=theta_view[c])
        g_raw = keep.tile([P, PACK, C_V], BF16)
        nc.sync.dma_start(out=g_raw[:], in_=g.rearrange("b (p t) v -> (b p) t v", t=PACK))
        x_sb = keep.tile([P, CH_TILES, QUERIES], BF16)
        x_view = x.rearrange("b (h p) f r s -> (b h) p (f r s)", p=P)
        w_sb = keep.tile([P, CH_TILES, C_V], BF16)
        for h in range(CH_TILES):
            if h == CH_TILES // 2:
                nc.sync.dma_start(out=w_sb[:], in_=w_attn_g.rearrange("(h p) v -> p h v", p=P))
            nc.sync.dma_start(out=x_sb[:, h, :], in_=x_view[h])

        ident_bf = keep.tile([P, P], BF16)
        make_identity(nc, ident_bf[:])
        ident_f32 = keep.tile([P, P], F32)
        make_identity(nc, ident_f32[:])

        warm = keep.tile([P, 1], F32)
        nc.scalar.activation(out=warm[:], in_=zero_col[:], func=ACT.Exp)

        def keep_busy(rhs, times):
            busy_ps = psum.tile([P, BANK], F32, tag="bank", name="busy_ps")
            for turn in range(times):
                nc.tensor.matmul(busy_ps[:], lhsT=ones[:], rhs=rhs, start=True, stop=True)

        keep_busy(ones[:].unsqueeze(1).to_broadcast([P, PACK, P]), 3)

        phiT = keep.tile([P, PACK, P], BF16)
        phiT_ps = psum.tile([P, PACK, P], BF16, tag="bank")
        for t in range(PACK):
            nc.tensor.transpose(phiT_ps[:, t, :], phi_sb[:, t, :], ident_bf[:])
        nc.vector.tensor_scalar_mul(out=phiT[:], in0=phiT_ps[:], scalar1=-1.0)

        thetaT = keep.tile([P, CHUNKS, PACK, P], BF16)
        soft = keep.tile([P, PACK, QUERIES], F32)
        neg_max = keep.tile([P, LAST, PACK], F32)
        neg_before = keep.tile([P, PACK], F32)
        neg_all = keep.tile([P, PACK], F32)
        sums = keep.tile([P, CHUNKS, PACK], F32)
        clipped = keep.tile([P, PACK, BANK], BF16)

        def transpose_theta(k):
            c = FRONT[k]
            thetaT_ps = psum.tile([P, PACK, P], BF16, tag="bank", name="thetaT_ps")
            for j in range(PACK):
                nc.tensor.transpose(thetaT_ps[:, j, :], theta_sb[:, c, j, :], ident_bf[:])
            if k < 3:
                nc.scalar.copy(out=thetaT[:, c, :, :], in_=thetaT_ps[:])
            else:
                nc.vector.tensor_copy(out=thetaT[:, c, :, :], in_=thetaT_ps[:])

        score_ps = {}

        def scores(k, t):
            s_ps = psum.tile([P, BANK], F32, tag="bank", name="s_ps")
            nc.tensor.matmul(
                s_ps[:],
                lhsT=phiT[:, t, :],
                rhs=thetaT[:, FRONT[k], :, :].rearrange("k j q -> k (j q)"),
                start=True,
                stop=True,
            )
            if k < LAST:
                bias = neg_max[:, k, t : t + 1]
                nc.vector.tensor_reduce(out=bias, in_=s_ps[:], axis=AX.X, op=ALU.min)
            else:
                bias = neg_all[:, t : t + 1]
                nc.vector.tensor_scalar(
                    out=clipped[:, t, :],
                    in0=s_ps[:],
                    scalar1=neg_before[:, t : t + 1],
                    scalar2=neg_max[:, LAST - 1, t : t + 1],
                    op0=ALU.min,
                    op1=ALU.min,
                    accum_out=bias,
                )
            score_ps[(k, t)] = (s_ps, bias)

        def exponential(k, t):
            s_ps, bias = score_ps[(k, t)]
            c = FRONT[k]
            nc.scalar.activation(
                out=soft[:, t, c * BANK : (c + 1) * BANK].rearrange("p (q j) -> p q j", j=PACK),
                in_=s_ps[:].rearrange("p (j q) -> p q j", j=PACK),
                func=ACT.Exp,
                bias=bias,
                scale=-1.0,
                accum_out=sums[:, k, t : t + 1],
            )

        transpose_theta(0)
        transpose_theta(1)
        g_grouped = keep.tile([P, PACK, P, PACK], BF16, align_bytes=64)
        nc.gpsimd.tensor_scalar(
            out=g_grouped[:],
            in0=g_raw[:].rearrange("p t (i u) -> p u i t", u=PACK),
            scalar1=1.0,
            scalar2=0.0,
            op0=ALU.mult,
            op1=ALU.add,
        )
        g_codes = keep.tile([P, C_V], U32, align_bytes=64)
        g_scales = keep.tile([P, C_V], U8, align_bytes=64)

        for t in range(PACK):
            scores(0, t)
            if t == 0:
                transpose_theta(2)
            exponential(0, t)
        gb_ps = psum.tile([P, CH_TILES + 2], F32, tag="bank")
        nc.tensor.matmul(gb_ps[:, 0:CH_TILES], lhsT=b_rows[:], rhs=ident_bf[:, 0:CH_TILES], start=True, stop=True)
        nc.tensor.matmul(gb_ps[:, CH_TILES:], lhsT=ones[:], rhs=gamma_row[:], start=True, stop=True)
        gb = keep.tile([P, CH_TILES + 2], F32)
        exp_neg_gamma = keep.tile([P, 1], F32)
        alpha = keep.tile([P, 1], F32)
        one_minus_alpha = keep.tile([P, 1], F32)
        for t in range(PACK):
            scores(1, t)
            if t == 0:
                nc.vector.tensor_copy(out=gb[:], in_=gb_ps[:])
            exponential(1, t)
            if t == 0:
                nc.scalar.activation(
                    out=exp_neg_gamma[:], in_=gb[:, CH_TILES : CH_TILES + 1], func=ACT.Exp, scale=-1.0
                )
            elif t == 2:
                nc.vector.tensor_scalar_add(out=alpha[:], in0=exp_neg_gamma[:], scalar1=1.0)
            elif t == 3:
                nc.vector.reciprocal(out=alpha[:], in_=alpha[:])
        nc.gpsimd.tensor_scalar(
            out=one_minus_alpha[:], in0=alpha[:], scalar1=-1.0, scalar2=1.0, op0=ALU.mult, op1=ALU.add
        )
        transpose_theta(3)
        for t in range(PACK):
            scores(2, t)
            exponential(2, t)
            if t == 1:
                nc.vector.tensor_tensor(out=neg_before[:], in0=neg_max[:, 0, :], in1=neg_max[:, 1, :], op=ALU.min)
        for t in range(PACK):
            scores(LAST, t)
            if t < PACK - 1:
                exponential(LAST, t)

        rescale = keep.tile([P, LAST, PACK], F32)
        nc.vector.tensor_tensor(
            out=rescale[:],
            in0=neg_all[:].unsqueeze(1).to_broadcast([P, LAST, PACK]),
            in1=neg_max[:],
            op=ALU.subtract,
        )
        nc.scalar.activation(out=rescale[:], in_=rescale[:], func=ACT.Exp)
        exponential(LAST, PACK - 1)

        nc.vector.quantize_mx(
            out=g_codes[:].bitcast(FP8X4),
            scales=g_scales[:],
            in_=g_grouped[:].rearrange("p u i t -> p (u i t)"),
        )
        scaled_sums = keep.tile([P, LAST, PACK], F32)
        nc.vector.tensor_tensor(out=scaled_sums[:], in0=rescale[:], in1=sums[:, 0:LAST, :], op=ALU.mult)
        key_sum = keep.tile([P, PACK], F32)
        nc.vector.tensor_reduce(
            out=key_sum[:], in_=scaled_sums[:].rearrange("p c t -> p t c"), axis=AX.X, op=ALU.add
        )
        nc.vector.tensor_add(out=key_sum[:], in0=key_sum[:], in1=sums[:, LAST, :])
        factor = keep.tile([P, CHUNKS, PACK], F32)
        nc.vector.reciprocal(out=factor[:, LAST, :], in_=key_sum[:])

        w_grouped = keep.tile([P, CH, PACK], BF16, align_bytes=64)
        w_words = w_grouped[:].bitcast(F32)
        w_codes = keep.tile([P, CH], U32, align_bytes=64)
        w_scales = keep.tile([P, CH], U8, align_bytes=64)
        wT = {}

        def transpose_w(pair):
            wT[pair] = psum.tile([P, 2, 2 * P], F32, tag="bank", name="wT_ps")
            for i in range(2):
                words = w_sb[:, 2 * pair + i, :].bitcast(F32).rearrange("p (q e) -> p e q", e=2)
                for e in range(2):
                    nc.tensor.transpose(wT[pair][:, e, i * P : (i + 1) * P], words[:, e, :], ident_f32[:])

        def copy_w(pair):
            nc.scalar.copy(
                out=w_words[:, 2 * pair * P : (2 * pair + 2) * P, :],
                in_=wT[pair][:].rearrange("q e o -> q o e"),
            )

        def quantise_w(half):
            cols = slice(half * CH // 2, (half + 1) * CH // 2)
            nc.vector.quantize_mx(
                out=w_codes[:, cols].bitcast(FP8X4),
                scales=w_scales[:, cols],
                in_=w_grouped[:, cols, :].rearrange("p o u -> p (o u)"),
            )

        attn_codes = keep.tile([P, QUERIES], U32, align_bytes=64)
        attn_scales = keep.tile([P, QUERIES], U8, align_bytes=64)
        a_codes = keep.tile([P, QUERIES], U32, align_bytes=64)
        a_scales = keep.tile([P, QUERIES], U8, align_bytes=64)
        out_view = out_0.rearrange("b (h p) f r s -> p (b h) (f r s)", p=P)
        attn_g_view = out_1.rearrange("b (h p) f r s -> p (b h) (f r s)", p=P)
        attn_grouped = {}
        a_grouped = {}

        def normalise(n0, width):
            k = FRONT.index(n0 // BANK)
            grouped = work.tile([P, 2 * P, PACK], BF16, align_bytes=64, name="attn_grouped")
            attn_grouped[n0] = grouped
            nc.vector.tensor_tensor(
                out=grouped[:, 0:width, :],
                in0=soft[:, :, n0 : n0 + width].rearrange("p t n -> p n t"),
                in1=factor[:, k, :].unsqueeze(1).to_broadcast([P, width, PACK]),
                op=ALU.mult,
            )

        def quantise_attn(n0, width):
            nc.vector.quantize_mx(
                out=attn_codes[:, n0 : n0 + width].bitcast(FP8X4),
                scales=attn_scales[:, n0 : n0 + width],
                in_=attn_grouped[n0][:, 0:width, :].rearrange("p n t -> p (n t)"),
            )

        def attend(n0, width):
            grouped = work.tile([P, 2 * P, PACK], BF16, align_bytes=64, name="a_grouped")
            a_grouped[n0] = grouped
            for nb in range(width // P):
                q0 = n0 + nb * P
                a_ps = psum.tile([P, PACK, P], F32, tag="bank", name="a_ps")
                for u in range(PACK):
                    nc.tensor.matmul_mx(
                        out=a_ps[:, u, :],
                        lhsT=g_codes[:, u * P : (u + 1) * P].bitcast(FP8X4),
                        lhsT_scale=g_scales[:, u * P : (u + 1) * P],
                        rhs=attn_codes[:, q0 : q0 + P].bitcast(FP8X4),
                        rhs_scale=attn_scales[:, q0 : q0 + P],
                        start=True,
                        stop=True,
                    )
                nc.scalar.copy(
                    out=grouped[:, nb * P : (nb + 1) * P, :],
                    in_=a_ps[:].rearrange("p u n -> p n u"),
                )

        def quantise_a(n0, width):
            nc.vector.quantize_mx(
                out=a_codes[:, n0 : n0 + width].bitcast(FP8X4),
                scales=a_scales[:, n0 : n0 + width],
                in_=a_grouped[n0][:, 0:width, :].rearrange("p n u -> p (n u)"),
            )

        mix_tile = {}
        attn_g_tile = {}

        def buffer(pool, views, n0, width, h):
            if (n0, h) not in views:
                tile = pool.tile([P, 2 * BANK], F32, name="%s_buffer" % ("mix" if pool is mixes else "attn_g"))
                share = 2 * BANK // width
                for i in range(share):
                    views[(n0, h - h % share + i)] = tile[:, i * width : (i + 1) * width]
            return views[(n0, h)]

        def scale_x(n0, width, h, engine):
            out = buffer(mixes, mix_tile, n0, width, h)
            in_ = x_sb[:, h, n0 : n0 + width]
            if engine == "scalar":
                nc.scalar.activation(out=out, in_=in_, func=ACT.Copy, scale=one_minus_alpha[:, 0:1])
            elif engine == "vector":
                nc.vector.tensor_scalar_mul(out=out, in0=in_, scalar1=one_minus_alpha[:, 0:1])
            else:
                nc.gpsimd.tensor_scalar(
                    out=out, in0=in_, scalar1=one_minus_alpha[:, 0:1], scalar2=0.0, op0=ALU.mult, op1=ALU.add
                )

        def project(n0, width, h):
            attn_g_sb = buffer(stage, attn_g_tile, n0, width, h)
            for m0 in range(n0, n0 + width, BANK):
                y_ps = psum.tile([P, BANK], F32, tag="bank", name="y_ps")
                nc.tensor.matmul_mx(
                    out=y_ps[:],
                    lhsT=w_codes[:, h * P : (h + 1) * P].bitcast(FP8X4),
                    lhsT_scale=w_scales[:, h * P : (h + 1) * P],
                    rhs=a_codes[:, m0 : m0 + BANK].bitcast(FP8X4),
                    rhs_scale=a_scales[:, m0 : m0 + BANK],
                    start=True,
                    stop=True,
                )
                nc.scalar.activation(
                    out=attn_g_sb[:, m0 - n0 : m0 - n0 + BANK],
                    in_=y_ps[:],
                    func=ACT.Identity,
                    bias=gb[:, h : h + 1],
                    scale=1.0,
                )
            nc.sync.dma_start(out=attn_g_view[:, h, n0 : n0 + width], in_=attn_g_sb)

        def project_half(n0, pair, half):
            m0 = n0 + half * 2 * P
            y_ps = psum.tile([P, 2, 2 * P], F32, tag="bank", name="y_ps")
            for i in range(2):
                h = 2 * pair + i
                nc.tensor.matmul_mx(
                    out=y_ps[:, i, :],
                    lhsT=w_codes[:, h * P : (h + 1) * P].bitcast(FP8X4),
                    lhsT_scale=w_scales[:, h * P : (h + 1) * P],
                    rhs=a_codes[:, m0 : m0 + 2 * P].bitcast(FP8X4),
                    rhs_scale=a_scales[:, m0 : m0 + 2 * P],
                    start=True,
                    stop=True,
                )
            for i in reversed(range(2)):
                h = 2 * pair + i
                piece = buffer(stage, attn_g_tile, n0, BANK, 2 * pair + i)[:, half * 2 * P : (half + 1) * 2 * P]
                nc.scalar.activation(
                    out=piece, in_=y_ps[:, i, :], func=ACT.Identity, bias=gb[:, h : h + 1], scale=1.0
                )
                nc.sync.dma_start(out=attn_g_view[:, h, m0 : m0 + 2 * P], in_=piece)

        def gate(n0, width, h):
            mixed = mix_tile[(n0, h)]
            nc.vector.scalar_tensor_tensor(
                out=mixed,
                in0=attn_g_tile[(n0, h)],
                scalar=alpha[:, 0:1],
                in1=mixed,
                op0=ALU.mult,
                op1=ALU.add,
            )
            nc.sync.dma_start(out=out_view[:, h, n0 : n0 + width], in_=mixed)

        UNIT = 2 * P
        for h in range(5):
            scale_x(0, BANK, h, "gpsimd")
        for pair in range(PAIRS):
            transpose_w(pair)
        for pair in range(PAIRS):
            copy_w(pair)
        keep_busy(clipped[:, PACK - 1, :], 5)
        for h in range(5, 6):
            scale_x(0, BANK, h, "scalar")
        for i in range(4):
            normalise(i * P, P)
            if i >= 1:
                quantise_attn((i - 1) * P, P)
                attend((i - 1) * P, P)
            if i >= 3:
                quantise_a((i - 3) * P, P)
        quantise_attn(3 * P, P)
        attend(3 * P, P)
        quantise_w(0)
        quantise_a(P, P)
        for pair in range(2):
            project_half(0, pair, 0)
        nc.vector.tensor_tensor(
            out=factor[:, 0:LAST, :],
            in0=rescale[:],
            in1=factor[:, LAST, :].unsqueeze(1).to_broadcast([P, LAST, PACK]),
            op=ALU.mult,
        )
        quantise_a(2 * P, P)
        quantise_a(3 * P, P)

        def prepare(n0):
            normalise(n0, UNIT)
            normalise(n0 + UNIT, UNIT)
            quantise_attn(n0, UNIT)
            quantise_attn(n0 + UNIT, UNIT)

        quantise_w(1)
        prepare(BANK)
        for pair in range(2):
            project_half(0, pair, 1)
        for h in range(4, CH_TILES):
            project(0, BANK, h)
        attend(BANK, UNIT)
        attend(BANK + UNIT, UNIT)
        for h in range(6):
            scale_x(BANK, BANK, h, "scalar")
        for h in range(6, CH_TILES):
            scale_x(0, BANK, h, "vector")
        for h in range(CH_TILES):
            gate(0, BANK, h)
            if h == 4:
                quantise_a(BANK, UNIT)
            if h == 6:
                quantise_a(BANK + UNIT, UNIT)
        prepare(2 * BANK)
        for h in range(CH_TILES):
            project(BANK, BANK, h)
        attend(2 * BANK, UNIT)
        attend(2 * BANK + UNIT, UNIT)
        prepare(3 * BANK)
        attend(3 * BANK, UNIT)
        attend(3 * BANK + UNIT, UNIT)
        for h in range(CH_TILES):
            gate(BANK, BANK, h)
            if h + 6 < CH_TILES:
                scale_x(BANK, BANK, h + 6, "vector")
            if h == 3:
                quantise_a(2 * BANK, UNIT)
                quantise_a(2 * BANK + UNIT, UNIT)
            if h == 5:
                quantise_a(3 * BANK, UNIT)
                quantise_a(3 * BANK + UNIT, UNIT)
        scale_x(2 * BANK, 2 * BANK, 0, "vector")
        for h in range(CH_TILES):
            project(2 * BANK, 2 * BANK, h)
            if h + 1 < CH_TILES:
                scale_x(2 * BANK, 2 * BANK, h + 1, "vector" if h % 2 else "scalar")
            gate(2 * BANK, 2 * BANK, h)
